import numpy as np
import ml_dtypes


def mxq(x, axis, fmt="e4m3"):
    dtype, down = {"e4m3": (ml_dtypes.float8_e4m3fn, 7), "e5m2": (ml_dtypes.float8_e5m2, 14)}[fmt]
    v = np.moveaxis(np.asarray(x, np.float32).astype(ml_dtypes.bfloat16).astype(np.float64), axis, -1)
    blocks = v.reshape(v.shape[:-1] + (-1, 32))
    amax = np.abs(blocks).max(-1, keepdims=True)
    byte = np.maximum(np.where(amax > 0, np.frexp(amax)[1] - 1 + 127, 0) - down, 1)
    scale = np.exp2(byte - 127.0)
    codes = (blocks / scale).astype(np.float32).astype(dtype).astype(np.float64)
    return np.moveaxis((codes * scale).reshape(v.shape), -1, axis)


WIDE = False


def mx_kscale(k):
    if not WIDE:
        return np.ones(k)
    levels = np.array([10, -10, 5, -5, 0])
    a = np.random.permutation(np.resize(levels, k // 512 * 4)).reshape(k // 512, 4)
    idx = np.arange(k)
    return np.exp2(a[idx // 512, idx % 128 // 32])


BF16 = ml_dtypes.bfloat16


def bf(x):
    return np.asarray(x, np.float32).astype(BF16)


def f64(x):
    return np.asarray(x).astype(np.float64)


B, T, N, F_IN, F_OUT, K = 1, 8, 1024, 512, 128, 4
D2, D3 = K - 2, K - 1


def delay(v, d):
    return np.concatenate([np.zeros((B, d, N, F_OUT)), v], axis=1)


def setup_inputs():
    s = mx_kscale(F_IN)
    return {"z2": bf(np.random.standard_normal((B, T - D2, N, F_IN)) * s),
            "S": bf(np.random.standard_normal((N, N)) / np.sqrt(N)),
            "w2": bf(np.random.standard_normal((F_OUT, F_IN)) / np.sqrt(F_IN) / s),
            "w3": bf(np.random.standard_normal((F_OUT, F_IN)) / np.sqrt(F_IN) / s),
            "y01": bf(np.random.standard_normal((B, T, N, F_OUT)) * 1.3),
            "b": bf(np.random.standard_normal(F_OUT) * 0.3)}


def reference(z2, S, w2, w3, y01, b):
    z2 = f64(z2)
    z3 = mxq(f64(S), 1, "e4m3") @ mxq(z2[:, :T - D3], 2, "e4m3")
    t2 = mxq(z2, 3, "e4m3") @ mxq(f64(w2), 1, "e4m3").T
    t3 = mxq(z3, 3, "e4m3") @ mxq(f64(w3), 1, "e4m3").T
    return f64(y01) + delay(t2, D2) + delay(t3, D3) + f64(b)

@@ -1,0 +1,318 @@
+from contextlib import ExitStack
+
+import concourse.bass as bass
+import concourse.mybir as mybir
+import concourse.tile as tile
+from concourse.masks import make_identity
+
+F32 = mybir.dt.float32
+BF16 = mybir.dt.bfloat16
+U32 = mybir.dt.uint32
+U8 = mybir.dt.uint8
+FP8X4 = mybir.dt.float8_e4m3fn_x4
+ADD = mybir.AluOpType.add
+
+P = 128
+T_OUT = 8
+T_Z2 = 6
+T_Z3 = 5
+NODES = 1024
+F_IN = 512
+F_OUT = 128
+
+FLOPS = 2 * (T_Z3 * NODES * NODES * F_IN + (T_Z2 + T_Z3) * NODES * F_IN * F_OUT)
+
+MANUAL = False
+RG_S = 0
+
+
+def tile_stgnnlayer_pb_t_kernel(tc, z2, S, w2, w3, y01, b, out):
+    nc = tc.nc
+    with ExitStack() as ctx:
+        const = ctx.enter_context(tc.tile_pool(name="const", bufs=1))
+        rot2 = ctx.enter_context(tc.tile_pool(name="rot2", bufs=2))
+        rot3 = ctx.enter_context(tc.tile_pool(name="rot3", bufs=3))
+        tpp = ctx.enter_context(tc.psum_pool(name="tpp", bufs=3))
+        z3p = ctx.enter_context(tc.psum_pool(name="z3p", bufs=3))
+        obp = ctx.enter_context(tc.psum_pool(name="obp", bufs=2))
+        if MANUAL:
+            ctx.enter_context(tc.manual_schedule())
+
+        ident_f = const.tile([P, P], F32, name="ident_f")
+        make_identity(nc, ident_f[:])
+        perm_f = const.tile([P, P], F32, name="perm_f")
+        nc.vector.tensor_copy(
+            out=perm_f[:].rearrange("p (s a) -> p s a", s=4),
+            in_=ident_f[:].rearrange("p (a s) -> p s a", s=4),
+        )
+        ident_b = const.tile([P, P], BF16, name="ident_b")
+        nc.vector.tensor_copy(out=ident_b[:], in_=ident_f[:])
+
+        zr = [const.tile([P, 8, F_IN], BF16, name="zr%d" % t) for t in range(T_Z2)]
+        sr = const.tile([P, 8, NODES], BF16, name="sr")
+        y01sb = const.tile([P, T_OUT, 8 * F_OUT], BF16, name="y01sb")
+        yb = const.tile([P, T_OUT, 8 * F_OUT], F32, name="yb")
+        w2sb = const.tile([P, F_IN], BF16, name="w2sb")
+        w3sb = const.tile([P, F_IN], BF16, name="w3sb")
+        bb = const.tile([P, F_OUT], BF16, name="bb")
+
+        def load_z(t, c_lo, c_hi):
+            src = z2[0, t].rearrange("(c p e) f -> p c e f", c=4, p=P, e=2)
+            dst = zr[t][:].rearrange("p (c e) f -> p c e f", e=2)
+            nc.sync.dma_start(out=dst[:, c_lo:c_hi], in_=src[:, c_lo:c_hi])
+
+        s_view = S.rearrange("(q r) m -> q r m", r=8)
+        y_view = y01[0].rearrange("t (q r) o -> q t (r o)", r=8)
+
+        nc.scalar.dma_start(out=w2sb[:], in_=w2)
+        nc.scalar.dma_start(out=w3sb[:], in_=w3)
+        load_z(0, 0, 2)
+        load_z(0, 2, 4)
+        for k in range(4):
+            nc.sync.dma_start(out=sr[:, 2 * k : 2 * k + 2, :], in_=s_view[:, 2 * k : 2 * k + 2, :])
+        load_z(1, 0, 4)
+        nc.sync.dma_start(out=bb[:], in_=b.partition_broadcast(P))
+        nc.sync.dma_start(out=y01sb[:, 0:4, :], in_=y_view[:, 0:4, :])
+        load_z(2, 0, 4)
+        nc.sync.dma_start(out=y01sb[:, 4:8, :], in_=y_view[:, 4:8, :])
+        load_z(3, 0, 4)
+        load_z(4, 0, 4)
+        load_z(5, 0, 4)
+
+        sqc = const.tile([P, 2048], U32, name="sqc", align_bytes=64)
+        sqs = const.tile([P, 2048], U8, name="sqs", align_bytes=64)
+        w2c = const.tile([P, P], U32, name="w2c", align_bytes=64)
+        w2s = const.tile([P, P], U8, name="w2s", align_bytes=64)
+        w3c = const.tile([P, P], U32, name="w3c", align_bytes=64)
+        w3s = const.tile([P, P], U8, name="w3s", align_bytes=64)
+        gm = {}
+        zmc = {}
+        zms = {}
+        gf = {}
+        zfc = {}
+        zfs = {}
+        g3 = {}
+        z3c = {}
+        z3s = {}
+        obs = {}
+
+        def evac(eng, dst, src):
+            if eng == "s":
+                nc.scalar.copy(out=dst, in_=src)
+            else:
+                nc.vector.tensor_copy(out=dst, in_=src)
+
+        srw = sr[:].bitcast(F32)
+
+        def s_chunk(k, engs):
+            gs = rot2.tile([P, 2048], BF16, tag="gs", name="gs%d" % k, align_bytes=64)
+            gsw = gs[:].bitcast(F32)
+            for g in range(2):
+                tb = tpp.tile([P, 512], F32, tag="tp", name="tbs%d_%d" % (k, g))
+                for u in range(2):
+                    for r2 in range(2):
+                        nc.tensor.transpose(
+                            tb[:, u * 256 + r2 * 128 : u * 256 + r2 * 128 + 128],
+                            srw[:, 2 * k + r2, (2 * g + u) * 128 : (2 * g + u) * 128 + 128],
+                            ident_f[:],
+                        )
+                evac(
+                    engs[g],
+                    gsw[:, g * 512 : (g + 1) * 512].rearrange("p (n u) -> p n u", u=2),
+                    tb[:].rearrange("p (u n) -> p n u", u=2),
+                )
+            return gs
+
+        def s_quant(k, gs):
+            nc.vector.quantize_mx(
+                out=sqc[:, k * 512 : (k + 1) * 512].bitcast(FP8X4),
+                scales=sqs[:, k * 512 : (k + 1) * 512],
+                in_=gs[:],
+            )
+
+        def w_prep():
+            gw2 = const.tile([P, F_IN], BF16, name="gw2", align_bytes=64)
+            gw3 = const.tile([P, F_IN], BF16, name="gw3", align_bytes=64)
+            tb2 = tpp.tile([P, 256], F32, tag="tp", name="tbw2")
+            w2w = w2sb[:].bitcast(F32)
+            for u in range(2):
+                nc.tensor.transpose(tb2[:, u * 128 : u * 128 + 128], w2w[:, u * 128 : u * 128 + 128], ident_f[:])
+            evac("s", gw2[:].bitcast(F32).rearrange("p (o u) -> p o u", u=2), tb2[:].rearrange("p (u o) -> p o u", u=2))
+            tb3 = tpp.tile([P, 512], BF16, tag="tp", name="tbw3")
+            for j in range(4):
+                nc.tensor.transpose(tb3[:, j * 128 : j * 128 + 128], w3sb[:, j * 128 : j * 128 + 128], ident_b[:])
+            evac("s", gw3[:].rearrange("p (o j) -> p o j", j=4), tb3[:].rearrange("p (j o) -> p o j", j=4))
+            nc.vector.quantize_mx(out=w2c[:].bitcast(FP8X4), scales=w2s[:], in_=gw2[:])
+            nc.vector.quantize_mx(out=w3c[:].bitcast(FP8X4), scales=w3s[:], in_=gw3[:])
+
+        def zf_alloc(t):
+            gf[t] = rot2.tile([P, 4096], BF16, tag="gf", name="gf%d" % t, align_bytes=64)
+            zfc[t] = rot3.tile([P, 1024], U32, tag="zfc", name="zfc%d" % t, align_bytes=64)
+            zfs[t] = rot3.tile([P, 1024], U8, tag="zfs", name="zfs%d" % t, align_bytes=64)
+
+        def zf_bank(t, c, eng):
+            zw = zr[t][:].bitcast(F32)
+            tb = tpp.tile([P, 512], F32, tag="tp", name="tbz%d_%d" % (t, c))
+            for u in range(2):
+                for e in range(2):
+                    nc.tensor.transpose(
+                        tb[:, u * 256 + e * 128 : u * 256 + e * 128 + 128],
+                        zw[:, 2 * c + e, u * 128 : u * 128 + 128],
+                        perm_f[:],
+                    )
+            gfw = gf[t][:].bitcast(F32).rearrange("p (r q u) -> p r q u", r=8, q=128, u=2)
+            evac(eng, gfw[:, :, 32 * c : 32 * c + 32, :], tb[:].rearrange("p (u r q) -> p r q u", u=2, r=8, q=32))
+
+        def zf_quant(t):
+            nc.vector.quantize_mx(out=zfc[t][:].bitcast(FP8X4), scales=zfs[t][:], in_=gf[t][:])
+
+        def zm_alloc(t):
+            gm[t] = rot2.tile([P, 2, 2048], BF16, tag="gm", name="gm%d" % t, align_bytes=64)
+            zmc[t] = rot2.tile([P, 1024], U32, tag="zmc", name="zmc%d" % t, align_bytes=64)
+            zms[t] = rot2.tile([P, 1024], U8, tag="zms", name="zms%d" % t, align_bytes=64)
+
+        def zm_regroup(t, g):
+            dst = gm[t][:, g, :].rearrange("p (c i j) -> p c j i", i=4, j=4)
+            src = zr[t][:, 4 * g : 4 * g + 4, :].rearrange("p j (c i) -> p c j i", i=4)
+            cv = (F_IN - RG_S) // 4
+            nc.vector.tensor_copy(out=dst[:, 0:cv], in_=src[:, 0:cv])
+            if RG_S:
+                nc.scalar.copy(out=dst[:, cv:128], in_=src[:, cv:128])
+
+        def zm_quant(t):
+            nc.vector.quantize_mx(
+                out=zmc[t][:].bitcast(FP8X4), scales=zms[t][:], in_=gm[t][:].rearrange("p g x -> p (g x)")
+            )
+
+        def z3_alloc(t):
+            g3[t] = rot2.tile([P, 8, 512], BF16, tag="g3", name="g3_%d" % t, align_bytes=64)
+            z3c[t] = rot2.tile([P, 1024], U32, tag="z3c", name="z3c%d" % t, align_bytes=64)
+            z3s[t] = rot2.tile([P, 1024], U8, tag="z3s", name="z3s%d" % t, align_bytes=64)
+
+        def z3_bank(t, r, eng):
+            zb = z3p.tile([P, 512], F32, tag="z3", name="zb%d_%d" % (t, r))
+            k, r2 = divmod(r, 2)
+            for j in range(4):
+                for g in range(2):
+                    a0 = g * 512 + j * 128
+                    b0 = k * 512 + g * 256 + r2 * 128
+                    nc.tensor.matmul_mx(
+                        out=zb[:, j * 128 : j * 128 + 128],
+                        lhsT=zmc[t][:, a0 : a0 + 128].bitcast(FP8X4),
+                        lhsT_scale=zms[t][:, a0 : a0 + 128],
+                        rhs=sqc[:, b0 : b0 + 128].bitcast(FP8X4),
+                        rhs_scale=sqs[:, b0 : b0 + 128],
+                        start=(g == 0),
+                        stop=(g == 1),
+                    )
+            evac(eng, g3[t][:, r, :].rearrange("p (q j) -> p q j", j=4), zb[:].rearrange("p (j q) -> p q j", j=4))
+
+        def z3_quant(t, h):
+            nc.vector.quantize_mx(
+                out=z3c[t][:, h * 512 : (h + 1) * 512].bitcast(FP8X4),
+                scales=z3s[t][:, h * 512 : (h + 1) * 512],
+                in_=g3[t][:, 4 * h : 4 * h + 4, :].rearrange("p r x -> p (r x)"),
+            )
+
+        def taps(tau, h):
+            ob = obp.tile([P, 512], F32, tag="ob", name="ob%d_%d" % (tau, h))
+            obs[(tau, h)] = ob
+            for i in range(4):
+                r = 4 * h + i
+                rp = (r % 2) * 4 + r // 2
+                nc.tensor.matmul_mx(
+                    out=ob[:, i * 128 : i * 128 + 128],
+                    lhsT=zfc[tau - 2][:, rp * 128 : rp * 128 + 128].bitcast(FP8X4),
+                    lhsT_scale=zfs[tau - 2][:, rp * 128 : rp * 128 + 128],
+                    rhs=w2c[:].bitcast(FP8X4),
+                    rhs_scale=w2s[:],
+                    start=True,
+                    stop=(tau < 3),
+                )
+                if tau >= 3:
+                    nc.tensor.matmul_mx(
+                        out=ob[:, i * 128 : i * 128 + 128],
+                        lhsT=z3c[tau - 3][:, r * 128 : r * 128 + 128].bitcast(FP8X4),
+                        lhsT_scale=z3s[tau - 3][:, r * 128 : r * 128 + 128],
+                        rhs=w3c[:].bitcast(FP8X4),
+                        rhs_scale=w3s[:],
+                        start=False,
+                        stop=True,
+                    )
+
+        def y_plus_b(tau):
+            nc.vector.tensor_tensor(
+                out=yb[:, tau, :].rearrange("p (r o) -> p r o", o=F_OUT),
+                in0=y01sb[:, tau, :].rearrange("p (r o) -> p r o", o=F_OUT),
+                in1=bb[:].unsqueeze(1).to_broadcast([P, 8, F_OUT]),
+                op=ADD,
+            )
+
+        def finish(tau, h):
+            nc.vector.tensor_tensor(
+                out=yb[:, tau, h * 512 : (h + 1) * 512],
+                in0=obs[(tau, h)][:],
+                in1=yb[:, tau, h * 512 : (h + 1) * 512],
+                op=ADD,
+            )
+
+        def store(tau, lo, hi):
+            o_view = out[0, tau].rearrange("(q r) o -> q (r o)", r=8)
+            nc.sync.dma_start(out=o_view[:, lo:hi], in_=yb[:, tau, lo:hi])
+
+        zf_alloc(0)
+        zm_alloc(0)
+        for c in range(4):
+            zf_bank(0, c, "s")
+        zm_regroup(0, 0)
+        zm_regroup(0, 1)
+        zm_quant(0)
+        gs_tiles = {}
+        for k in range(4):
+            gs_tiles[k] = s_chunk(k, ("s", "v"))
+            s_quant(k, gs_tiles[k])
+            if k == 0:
+                zf_quant(0)
+            if k == 1:
+                w_prep()
+
+        yb_plan = {0: (2, 3), 1: (4, 5), 2: (6, 7), 3: (0,), 4: (1,)}
+        for t in range(T_Z3):
+            if t > 0:
+                z3_quant(t - 1, 1)
+            if t + 1 >= 2:
+                finish(t + 1, 0)
+                finish(t + 1, 1)
+                store(t + 1, 0, 1024)
+            z3_alloc(t)
+            for r in range(4):
+                z3_bank(t, r, "s")
+            if t + 1 < T_Z3:
+                zm_alloc(t + 1)
+                zm_regroup(t + 1, 0)
+                zm_regroup(t + 1, 1)
+            zf_alloc(t + 1)
+            for c in range(4):
+                zf_bank(t + 1, c, "s")
+            z3_quant(t, 0)
+            if t + 1 < T_Z3:
+                zm_quant(t + 1)
+            for tau in yb_plan[t]:
+                y_plus_b(tau)
+                if tau < 2:
+                    store(tau, 0, 1024)
+            for r in range(4, 8):
+                z3_bank(t, r, "s")
+            zf_quant(t + 1)
+            taps(t + 2, 0)
+            taps(t + 2, 1)
+        z3_quant(4, 1)
+        finish(6, 0)
+        finish(6, 1)
+        store(6, 0, 1024)
+        taps(7, 0)
+        taps(7, 1)
+        finish(7, 0)
+        store(7, 0, 512)
+        finish(7, 1)
+        store(7, 512, 1024)

@@ -22,8 +22,8 @@ F_OUT = 128
 
 FLOPS = 2 * (T_Z3 * NODES * NODES * F_IN + (T_Z2 + T_Z3) * NODES * F_IN * F_OUT)
 
-MANUAL = False
-RG_S = 0
+MANUAL = True
+RG_S = 256
 
 
 def tile_stgnnlayer_pb_t_kernel(tc, z2, S, w2, w3, y01, b, out):
@@ -64,13 +64,13 @@ def tile_stgnnlayer_pb_t_kernel(tc, z2, S, w2, w3, y01, b, out):
         s_view = S.rearrange("(q r) m -> q r m", r=8)
         y_view = y01[0].rearrange("t (q r) o -> q t (r o)", r=8)
 
-        nc.scalar.dma_start(out=w2sb[:], in_=w2)
-        nc.scalar.dma_start(out=w3sb[:], in_=w3)
         load_z(0, 0, 2)
         load_z(0, 2, 4)
         for k in range(4):
             nc.sync.dma_start(out=sr[:, 2 * k : 2 * k + 2, :], in_=s_view[:, 2 * k : 2 * k + 2, :])
         load_z(1, 0, 4)
+        nc.sync.dma_start(out=w2sb[:], in_=w2)
+        nc.sync.dma_start(out=w3sb[:], in_=w3)
         nc.sync.dma_start(out=bb[:], in_=b.partition_broadcast(P))
         nc.sync.dma_start(out=y01sb[:, 0:4, :], in_=y_view[:, 0:4, :])
         load_z(2, 0, 4)
@@ -104,35 +104,38 @@ def tile_stgnnlayer_pb_t_kernel(tc, z2, S, w2, w3, y01, b, out):
 
         srw = sr[:].bitcast(F32)
 
-        def s_chunk(k, engs):
-            gs = rot2.tile([P, 2048], BF16, tag="gs", name="gs%d" % k, align_bytes=64)
-            gsw = gs[:].bitcast(F32)
-            for g in range(2):
-                tb = tpp.tile([P, 512], F32, tag="tp", name="tbs%d_%d" % (k, g))
-                for u in range(2):
-                    for r2 in range(2):
-                        nc.tensor.transpose(
-                            tb[:, u * 256 + r2 * 128 : u * 256 + r2 * 128 + 128],
-                            srw[:, 2 * k + r2, (2 * g + u) * 128 : (2 * g + u) * 128 + 128],
-                            ident_f[:],
-                        )
-                evac(
-                    engs[g],
-                    gsw[:, g * 512 : (g + 1) * 512].rearrange("p (n u) -> p n u", u=2),
-                    tb[:].rearrange("p (u n) -> p n u", u=2),
-                )
-            return gs
+        gs_tiles = {}
 
-        def s_quant(k, gs):
+        def s_bank(k, g, eng):
+            if g == 0:
+                gs_tiles[k] = rot2.tile([P, 2048], BF16, tag="gs", name="gs%d" % k, align_bytes=64)
+            gsw = gs_tiles[k][:].bitcast(F32)
+            tb = tpp.tile([P, 512], F32, tag="tp", name="tbs%d_%d" % (k, g))
+            for u in range(2):
+                for r2 in range(2):
+                    nc.tensor.transpose(
+                        tb[:, u * 256 + r2 * 128 : u * 256 + r2 * 128 + 128],
+                        srw[:, 2 * k + r2, (2 * g + u) * 128 : (2 * g + u) * 128 + 128],
+                        ident_f[:],
+                    )
+            evac(
+                eng,
+                gsw[:, g * 512 : (g + 1) * 512].rearrange("p (n u) -> p n u", u=2),
+                tb[:].rearrange("p (u n) -> p n u", u=2),
+            )
+
+        def s_quant(k):
+            gs = gs_tiles[k]
             nc.vector.quantize_mx(
                 out=sqc[:, k * 512 : (k + 1) * 512].bitcast(FP8X4),
                 scales=sqs[:, k * 512 : (k + 1) * 512],
                 in_=gs[:],
             )
 
-        def w_prep():
-            gw2 = const.tile([P, F_IN], BF16, name="gw2", align_bytes=64)
-            gw3 = const.tile([P, F_IN], BF16, name="gw3", align_bytes=64)
+        gw2 = const.tile([P, F_IN], BF16, name="gw2", align_bytes=64)
+        gw3 = const.tile([P, F_IN], BF16, name="gw3", align_bytes=64)
+
+        def w_tr():
             tb2 = tpp.tile([P, 256], F32, tag="tp", name="tbw2")
             w2w = w2sb[:].bitcast(F32)
             for u in range(2):
@@ -142,6 +145,8 @@ def tile_stgnnlayer_pb_t_kernel(tc, z2, S, w2, w3, y01, b, out):
             for j in range(4):
                 nc.tensor.transpose(tb3[:, j * 128 : j * 128 + 128], w3sb[:, j * 128 : j * 128 + 128], ident_b[:])
             evac("s", gw3[:].rearrange("p (o j) -> p o j", j=4), tb3[:].rearrange("p (j o) -> p o j", j=4))
+
+        def w_quant():
             nc.vector.quantize_mx(out=w2c[:].bitcast(FP8X4), scales=w2s[:], in_=gw2[:])
             nc.vector.quantize_mx(out=w3c[:].bitcast(FP8X4), scales=w3s[:], in_=gw3[:])
 
@@ -171,13 +176,20 @@ def tile_stgnnlayer_pb_t_kernel(tc, z2, S, w2, w3, y01, b, out):
             zmc[t] = rot2.tile([P, 1024], U32, tag="zmc", name="zmc%d" % t, align_bytes=64)
             zms[t] = rot2.tile([P, 1024], U8, tag="zms", name="zms%d" % t, align_bytes=64)
 
-        def zm_regroup(t, g):
+        def zm_views(t, g):
             dst = gm[t][:, g, :].rearrange("p (c i j) -> p c j i", i=4, j=4)
             src = zr[t][:, 4 * g : 4 * g + 4, :].rearrange("p j (c i) -> p c j i", i=4)
-            cv = (F_IN - RG_S) // 4
+            return dst, src
+
+        def rg_v(t, g, xs):
+            dst, src = zm_views(t, g)
+            cv = (F_IN - xs) // 4
             nc.vector.tensor_copy(out=dst[:, 0:cv], in_=src[:, 0:cv])
-            if RG_S:
-                nc.scalar.copy(out=dst[:, cv:128], in_=src[:, cv:128])
+
+        def rg_s(t, g, xs):
+            dst, src = zm_views(t, g)
+            cv = (F_IN - xs) // 4
+            nc.scalar.copy(out=dst[:, cv:128], in_=src[:, cv:128])
 
         def zm_quant(t):
             nc.vector.quantize_mx(
@@ -207,11 +219,11 @@ def tile_stgnnlayer_pb_t_kernel(tc, z2, S, w2, w3, y01, b, out):
                     )
             evac(eng, g3[t][:, r, :].rearrange("p (q j) -> p q j", j=4), zb[:].rearrange("p (j q) -> p q j", j=4))
 
-        def z3_quant(t, h):
+        def z3_quant(t, r_lo, r_hi):
             nc.vector.quantize_mx(
-                out=z3c[t][:, h * 512 : (h + 1) * 512].bitcast(FP8X4),
-                scales=z3s[t][:, h * 512 : (h + 1) * 512],
-                in_=g3[t][:, 4 * h : 4 * h + 4, :].rearrange("p r x -> p (r x)"),
+                out=z3c[t][:, r_lo * 128 : r_hi * 128].bitcast(FP8X4),
+                scales=z3s[t][:, r_lo * 128 : r_hi * 128],
+                in_=g3[t][:, r_lo:r_hi, :].rearrange("p r x -> p (r x)"),
             )
 
         def taps(tau, h):
@@ -264,50 +276,69 @@ def tile_stgnnlayer_pb_t_kernel(tc, z2, S, w2, w3, y01, b, out):
         zm_alloc(0)
         for c in range(4):
             zf_bank(0, c, "s")
-        zm_regroup(0, 0)
-        zm_regroup(0, 1)
+        rg_v(0, 0, 0)
+        rg_v(0, 1, 0)
         zm_quant(0)
-        gs_tiles = {}
+        zm_alloc(1)
+        z3_alloc(0)
         for k in range(4):
-            gs_tiles[k] = s_chunk(k, ("s", "v"))
-            s_quant(k, gs_tiles[k])
+            s_bank(k, 0, "s")
+            s_bank(k, 1, "s")
+            s_quant(k)
             if k == 0:
                 zf_quant(0)
-            if k == 1:
-                w_prep()
+        for r in range(4):
+            z3_bank(0, r, "s")
 
         yb_plan = {0: (2, 3), 1: (4, 5), 2: (6, 7), 3: (0,), 4: (1,)}
         for t in range(T_Z3):
+            last = t == T_Z3 - 1
             if t > 0:
-                z3_quant(t - 1, 1)
+                z3_quant(t - 1, 4, 8)
             if t + 1 >= 2:
                 finish(t + 1, 0)
                 finish(t + 1, 1)
                 store(t + 1, 0, 1024)
-            z3_alloc(t)
-            for r in range(4):
-                z3_bank(t, r, "s")
-            if t + 1 < T_Z3:
-                zm_alloc(t + 1)
-                zm_regroup(t + 1, 0)
-                zm_regroup(t + 1, 1)
-            zf_alloc(t + 1)
-            for c in range(4):
-                zf_bank(t + 1, c, "s")
-            z3_quant(t, 0)
-            if t + 1 < T_Z3:
+            if t > 0:
+                z3_alloc(t)
+            if last:
+                zf_alloc(5)
+                for c in range(4):
+                    zf_bank(5, c, "s")
+            if t > 0:
+                for r in range(4):
+                    z3_bank(t, r, "s")
+            if not last:
+                rg_v(t + 1, 0, 0)
+                rg_v(t + 1, 1, RG_S if t > 0 else 0)
+                zf_alloc(t + 1)
+                for c in range(4):
+                    zf_bank(t + 1, c, "s")
+            if t == 0:
+                w_tr()
+            if last:
+                zf_quant(5)
+            z3_quant(t, 0, 4)
+            if not last:
                 zm_quant(t + 1)
+            if t == 0:
+                w_quant()
             for tau in yb_plan[t]:
                 y_plus_b(tau)
                 if tau < 2:
                     store(tau, 0, 1024)
             for r in range(4, 8):
                 z3_bank(t, r, "s")
-            zf_quant(t + 1)
+            if t + 2 < T_Z3:
+                zm_alloc(t + 2)
+                rg_s(t + 2, 1, RG_S)
+            if not last:
+                zf_quant(t + 1)
             taps(t + 2, 0)
             taps(t + 2, 1)
-        z3_quant(4, 1)
+        z3_quant(4, 4, 6)
         finish(6, 0)
+        z3_quant(4, 6, 8)
         finish(6, 1)
         store(6, 0, 1024)
         taps(7, 0)

@@ -38,6 +38,10 @@ def tile_stgnnlayer_pb_t_kernel(tc, z2, S, w2, w3, y01, b, out):
         if MANUAL:
             ctx.enter_context(tc.manual_schedule())
 
+        brow = const.tile([P, F_OUT], BF16, name="brow")
+        ones = const.tile([P, P], BF16, name="ones")
+        nc.vector.memset(brow[:], 0.0)
+        nc.vector.memset(ones[:], 1.0)
         ident_f = const.tile([P, P], F32, name="ident_f")
         make_identity(nc, ident_f[:])
         perm_f = const.tile([P, P], F32, name="perm_f")
@@ -54,7 +58,7 @@ def tile_stgnnlayer_pb_t_kernel(tc, z2, S, w2, w3, y01, b, out):
         yb = const.tile([P, T_OUT, 8 * F_OUT], F32, name="yb")
         w2sb = const.tile([P, F_IN], BF16, name="w2sb")
         w3sb = const.tile([P, F_IN], BF16, name="w3sb")
-        bb = const.tile([P, F_OUT], BF16, name="bb")
+        bb = const.tile([P, F_OUT], F32, name="bb")
 
         def load_z(t, c_lo, c_hi):
             src = z2[0, t].rearrange("(c p e) f -> p c e f", c=4, p=P, e=2)
@@ -64,14 +68,14 @@ def tile_stgnnlayer_pb_t_kernel(tc, z2, S, w2, w3, y01, b, out):
         s_view = S.rearrange("(q r) m -> q r m", r=8)
         y_view = y01[0].rearrange("t (q r) o -> q t (r o)", r=8)
 
-        load_z(0, 0, 2)
-        load_z(0, 2, 4)
+        for c in range(4):
+            load_z(0, c, c + 1)
+        nc.sync.dma_start(out=brow[0:1, :], in_=b.unsqueeze(0))
         for k in range(4):
             nc.sync.dma_start(out=sr[:, 2 * k : 2 * k + 2, :], in_=s_view[:, 2 * k : 2 * k + 2, :])
         load_z(1, 0, 4)
         nc.sync.dma_start(out=w2sb[:], in_=w2)
         nc.sync.dma_start(out=w3sb[:], in_=w3)
-        nc.sync.dma_start(out=bb[:], in_=b.partition_broadcast(P))
         nc.sync.dma_start(out=y01sb[:, 0:4, :], in_=y_view[:, 0:4, :])
         load_z(2, 0, 4)
         nc.sync.dma_start(out=y01sb[:, 4:8, :], in_=y_view[:, 4:8, :])
@@ -149,6 +153,11 @@ def tile_stgnnlayer_pb_t_kernel(tc, z2, S, w2, w3, y01, b, out):
         def w_quant():
             nc.vector.quantize_mx(out=w2c[:].bitcast(FP8X4), scales=w2s[:], in_=gw2[:])
             nc.vector.quantize_mx(out=w3c[:].bitcast(FP8X4), scales=w3s[:], in_=gw3[:])
+
+        def bias_spread():
+            pb = tpp.tile([P, F_OUT], F32, tag="tp", name="pb")
+            nc.tensor.matmul(out=pb[:], lhsT=ones[:], rhs=brow[:], start=True, stop=True)
+            evac("s", bb[:], pb[:])
 
         def zf_alloc(t):
             gf[t] = rot2.tile([P, 4096], BF16, tag="gf", name="gf%d" % t, align_bytes=64)
@@ -276,6 +285,7 @@ def tile_stgnnlayer_pb_t_kernel(tc, z2, S, w2, w3, y01, b, out):
         zm_alloc(0)
         for c in range(4):
             zf_bank(0, c, "s")
+        bias_spread()
         rg_v(0, 0, 0)
         rg_v(0, 1, 0)
         zm_quant(0)

@@ -23,7 +23,7 @@ F_OUT = 128
 FLOPS = 2 * (T_Z3 * NODES * NODES * F_IN + (T_Z2 + T_Z3) * NODES * F_IN * F_OUT)
 
 MANUAL = True
-RG_S = 256
+RG_S = 192
 
 
 def tile_stgnnlayer_pb_t_kernel(tc, z2, S, w2, w3, y01, b, out):
@@ -235,11 +235,11 @@ def tile_stgnnlayer_pb_t_kernel(tc, z2, S, w2, w3, y01, b, out):
                 in_=g3[t][:, r_lo:r_hi, :].rearrange("p r x -> p (r x)"),
             )
 
-        def taps(tau, h):
-            ob = obp.tile([P, 512], F32, tag="ob", name="ob%d_%d" % (tau, h))
-            obs[(tau, h)] = ob
-            for i in range(4):
-                r = 4 * h + i
+        def taps(tau, r_lo, r_hi, pool, tag):
+            ob = pool.tile([P, (r_hi - r_lo) * 128], F32, tag=tag, name="ob%d_%d" % (tau, r_lo))
+            obs[(tau, r_lo)] = ob
+            for r in range(r_lo, r_hi):
+                i = r - r_lo
                 rp = (r % 2) * 4 + r // 2
                 nc.tensor.matmul_mx(
                     out=ob[:, i * 128 : i * 128 + 128],
@@ -269,11 +269,11 @@ def tile_stgnnlayer_pb_t_kernel(tc, z2, S, w2, w3, y01, b, out):
                 op=ADD,
             )
 
-        def finish(tau, h):
+        def finish(tau, r_lo, r_hi):
             nc.vector.tensor_tensor(
-                out=yb[:, tau, h * 512 : (h + 1) * 512],
-                in0=obs[(tau, h)][:],
-                in1=yb[:, tau, h * 512 : (h + 1) * 512],
+                out=yb[:, tau, r_lo * 128 : r_hi * 128],
+                in0=obs[(tau, r_lo)][:],
+                in1=yb[:, tau, r_lo * 128 : r_hi * 128],
                 op=ADD,
             )
 
@@ -295,65 +295,78 @@ def tile_stgnnlayer_pb_t_kernel(tc, z2, S, w2, w3, y01, b, out):
             s_bank(k, 0, "s")
             s_bank(k, 1, "s")
             s_quant(k)
-            if k == 0:
+            if k == 1:
                 zf_quant(0)
         for r in range(4):
             z3_bank(0, r, "s")
 
-        yb_plan = {0: (2, 3), 1: (4, 5), 2: (6, 7), 3: (0,), 4: (1,)}
-        for t in range(T_Z3):
-            last = t == T_Z3 - 1
+        yb_plan = {0: (2, 3), 1: (4, 5), 2: (6, 0), 3: (7, 1)}
+        for t in range(T_Z3 - 1):
             if t > 0:
                 z3_quant(t - 1, 4, 8)
             if t + 1 >= 2:
-                finish(t + 1, 0)
-                finish(t + 1, 1)
+                finish(t + 1, 0, 4)
+                finish(t + 1, 4, 8)
                 store(t + 1, 0, 1024)
             if t > 0:
                 z3_alloc(t)
-            if last:
-                zf_alloc(5)
-                for c in range(4):
-                    zf_bank(5, c, "s")
-            if t > 0:
                 for r in range(4):
                     z3_bank(t, r, "s")
-            if not last:
-                rg_v(t + 1, 0, 0)
-                rg_v(t + 1, 1, RG_S if t > 0 else 0)
-                zf_alloc(t + 1)
-                for c in range(4):
-                    zf_bank(t + 1, c, "s")
+            rg_v(t + 1, 0, 0)
+            rg_v(t + 1, 1, RG_S if t > 0 else 0)
+            zf_alloc(t + 1)
+            for c in range(4):
+                zf_bank(t + 1, c, "s")
             if t == 0:
                 w_tr()
-            if last:
-                zf_quant(5)
             z3_quant(t, 0, 4)
-            if not last:
-                zm_quant(t + 1)
-            if t == 0:
-                w_quant()
+            zm_quant(t + 1)
             for tau in yb_plan[t]:
                 y_plus_b(tau)
                 if tau < 2:
                     store(tau, 0, 1024)
+            if t == 0:
+                w_quant()
             for r in range(4, 8):
                 z3_bank(t, r, "s")
             if t + 2 < T_Z3:
                 zm_alloc(t + 2)
                 rg_s(t + 2, 1, RG_S)
-            if not last:
-                zf_quant(t + 1)
-            taps(t + 2, 0)
-            taps(t + 2, 1)
+            zf_quant(t + 1)
+            taps(t + 2, 0, 4, obp, "ob")
+            taps(t + 2, 4, 8, obp, "ob")
+
+        z3_quant(3, 4, 8)
+        finish(5, 0, 4)
+        finish(5, 4, 8)
+        store(5, 0, 1024)
+        z3_alloc(4)
+        zf_alloc(5)
+        for c in range(4):
+            zf_bank(5, c, "s")
+        for r in range(4):
+            z3_bank(4, r, "s")
+        zf_quant(5)
+        z3_quant(4, 0, 4)
+        z3_bank(4, 4, "s")
+        z3_bank(4, 5, "s")
+        taps(6, 0, 4, obp, "ob")
+        z3_bank(4, 6, "s")
+        taps(6, 4, 8, obp, "ob")
+        z3_bank(4, 7, "s")
         z3_quant(4, 4, 6)
-        finish(6, 0)
-        z3_quant(4, 6, 8)
-        finish(6, 1)
+        finish(6, 0, 4)
+        taps(7, 0, 4, tpp, "tp")
+        z3_quant(4, 6, 7)
+        finish(6, 4, 8)
         store(6, 0, 1024)
-        taps(7, 0)
-        taps(7, 1)
-        finish(7, 0)
-        store(7, 0, 512)
-        finish(7, 1)
-        store(7, 512, 1024)
+        taps(7, 4, 6, tpp, "tp")
+        z3_quant(4, 7, 8)
+        taps(7, 6, 7, tpp, "tp")
+        finish(7, 0, 4)
+        taps(7, 7, 8, obp, "ob")
+        finish(7, 4, 6)
+        store(7, 0, 768)
+        finish(7, 6, 7)
+        finish(7, 7, 8)
+        store(7, 768, 1024)

@@ -23,7 +23,7 @@ F_OUT = 128
 FLOPS = 2 * (T_Z3 * NODES * NODES * F_IN + (T_Z2 + T_Z3) * NODES * F_IN * F_OUT)
 
 MANUAL = True
-RG_S = 192
+RG_S = 320
 
 
 def tile_stgnnlayer_pb_t_kernel(tc, z2, S, w2, w3, y01, b, out):
@@ -32,9 +32,7 @@ def tile_stgnnlayer_pb_t_kernel(tc, z2, S, w2, w3, y01, b, out):
         const = ctx.enter_context(tc.tile_pool(name="const", bufs=1))
         rot2 = ctx.enter_context(tc.tile_pool(name="rot2", bufs=2))
         rot3 = ctx.enter_context(tc.tile_pool(name="rot3", bufs=3))
-        tpp = ctx.enter_context(tc.psum_pool(name="tpp", bufs=3))
-        z3p = ctx.enter_context(tc.psum_pool(name="z3p", bufs=3))
-        obp = ctx.enter_context(tc.psum_pool(name="obp", bufs=2))
+        psp = ctx.enter_context(tc.psum_pool(name="psp", bufs=8))
         if MANUAL:
             ctx.enter_context(tc.manual_schedule())
 
@@ -73,13 +71,15 @@ def tile_stgnnlayer_pb_t_kernel(tc, z2, S, w2, w3, y01, b, out):
         nc.sync.dma_start(out=brow[0:1, :], in_=b.unsqueeze(0))
         for k in range(4):
             nc.sync.dma_start(out=sr[:, 2 * k : 2 * k + 2, :], in_=s_view[:, 2 * k : 2 * k + 2, :])
+            if k == 1:
+                nc.sync.dma_start(out=w2sb[:], in_=w2)
+                nc.sync.dma_start(out=w3sb[:], in_=w3)
         load_z(1, 0, 4)
-        nc.sync.dma_start(out=w2sb[:], in_=w2)
-        nc.sync.dma_start(out=w3sb[:], in_=w3)
-        nc.sync.dma_start(out=y01sb[:, 0:4, :], in_=y_view[:, 0:4, :])
+        nc.sync.dma_start(out=y01sb[:, 2:4, :], in_=y_view[:, 2:4, :])
         load_z(2, 0, 4)
         nc.sync.dma_start(out=y01sb[:, 4:8, :], in_=y_view[:, 4:8, :])
         load_z(3, 0, 4)
+        nc.sync.dma_start(out=y01sb[:, 0:2, :], in_=y_view[:, 0:2, :])
         load_z(4, 0, 4)
         load_z(5, 0, 4)
 
@@ -114,7 +114,7 @@ def tile_stgnnlayer_pb_t_kernel(tc, z2, S, w2, w3, y01, b, out):
             if g == 0:
                 gs_tiles[k] = rot2.tile([P, 2048], BF16, tag="gs", name="gs%d" % k, align_bytes=64)
             gsw = gs_tiles[k][:].bitcast(F32)
-            tb = tpp.tile([P, 512], F32, tag="tp", name="tbs%d_%d" % (k, g))
+            tb = psp.tile([P, 512], F32, tag="ps", name="tbs%d_%d" % (k, g))
             for u in range(2):
                 for r2 in range(2):
                     nc.tensor.transpose(
@@ -140,12 +140,12 @@ def tile_stgnnlayer_pb_t_kernel(tc, z2, S, w2, w3, y01, b, out):
         gw3 = const.tile([P, F_IN], BF16, name="gw3", align_bytes=64)
 
         def w_tr():
-            tb2 = tpp.tile([P, 256], F32, tag="tp", name="tbw2")
+            tb2 = psp.tile([P, 256], F32, tag="ps", name="tbw2")
             w2w = w2sb[:].bitcast(F32)
             for u in range(2):
                 nc.tensor.transpose(tb2[:, u * 128 : u * 128 + 128], w2w[:, u * 128 : u * 128 + 128], ident_f[:])
             evac("s", gw2[:].bitcast(F32).rearrange("p (o u) -> p o u", u=2), tb2[:].rearrange("p (u o) -> p o u", u=2))
-            tb3 = tpp.tile([P, 512], BF16, tag="tp", name="tbw3")
+            tb3 = psp.tile([P, 512], BF16, tag="ps", name="tbw3")
             for j in range(4):
                 nc.tensor.transpose(tb3[:, j * 128 : j * 128 + 128], w3sb[:, j * 128 : j * 128 + 128], ident_b[:])
             evac("s", gw3[:].rearrange("p (o j) -> p o j", j=4), tb3[:].rearrange("p (j o) -> p o j", j=4))
@@ -155,7 +155,7 @@ def tile_stgnnlayer_pb_t_kernel(tc, z2, S, w2, w3, y01, b, out):
             nc.vector.quantize_mx(out=w3c[:].bitcast(FP8X4), scales=w3s[:], in_=gw3[:])
 
         def bias_spread():
-            pb = tpp.tile([P, F_OUT], F32, tag="tp", name="pb")
+            pb = psp.tile([P, F_OUT], F32, tag="ps", name="pb")
             nc.tensor.matmul(out=pb[:], lhsT=ones[:], rhs=brow[:], start=True, stop=True)
             evac("s", bb[:], pb[:])
 
@@ -166,7 +166,7 @@ def tile_stgnnlayer_pb_t_kernel(tc, z2, S, w2, w3, y01, b, out):
 
         def zf_bank(t, c, eng):
             zw = zr[t][:].bitcast(F32)
-            tb = tpp.tile([P, 512], F32, tag="tp", name="tbz%d_%d" % (t, c))
+            tb = psp.tile([P, 512], F32, tag="ps", name="tbz%d_%d" % (t, c))
             for u in range(2):
                 for e in range(2):
                     nc.tensor.transpose(
@@ -211,7 +211,7 @@ def tile_stgnnlayer_pb_t_kernel(tc, z2, S, w2, w3, y01, b, out):
             z3s[t] = rot2.tile([P, 1024], U8, tag="z3s", name="z3s%d" % t, align_bytes=64)
 
         def z3_bank(t, r, eng):
-            zb = z3p.tile([P, 512], F32, tag="z3", name="zb%d_%d" % (t, r))
+            zb = psp.tile([P, 512], F32, tag="ps", name="zb%d_%d" % (t, r))
             k, r2 = divmod(r, 2)
             for j in range(4):
                 for g in range(2):
@@ -235,8 +235,8 @@ def tile_stgnnlayer_pb_t_kernel(tc, z2, S, w2, w3, y01, b, out):
                 in_=g3[t][:, r_lo:r_hi, :].rearrange("p r x -> p (r x)"),
             )
 
-        def taps(tau, r_lo, r_hi, pool, tag):
-            ob = pool.tile([P, (r_hi - r_lo) * 128], F32, tag=tag, name="ob%d_%d" % (tau, r_lo))
+        def taps(tau, r_lo, r_hi):
+            ob = psp.tile([P, (r_hi - r_lo) * 128], F32, tag="ps", name="ob%d_%d" % (tau, r_lo))
             obs[(tau, r_lo)] = ob
             for r in range(r_lo, r_hi):
                 i = r - r_lo
@@ -297,74 +297,56 @@ def tile_stgnnlayer_pb_t_kernel(tc, z2, S, w2, w3, y01, b, out):
             s_quant(k)
             if k == 1:
                 zf_quant(0)
-        for r in range(4):
-            z3_bank(0, r, "s")
+            if k == 2:
+                w_tr()
+                w_quant()
 
-        yb_plan = {0: (2, 3), 1: (4, 5), 2: (6, 0), 3: (7, 1)}
-        for t in range(T_Z3 - 1):
+        yb_plan = {0: (), 1: (4, 5), 2: (6, 0), 3: (7, 1), 4: ()}
+        for t in range(T_Z3):
+            last = t == T_Z3 - 1
             if t > 0:
                 z3_quant(t - 1, 4, 8)
-            if t + 1 >= 2:
-                finish(t + 1, 0, 4)
-                finish(t + 1, 4, 8)
-                store(t + 1, 0, 1024)
-            if t > 0:
                 z3_alloc(t)
-                for r in range(4):
-                    z3_bank(t, r, "s")
-            rg_v(t + 1, 0, 0)
-            rg_v(t + 1, 1, RG_S if t > 0 else 0)
+            for r in range(4):
+                z3_bank(t, r, "s")
+            if not last:
+                rg_v(t + 1, 0, 0)
+                rg_v(t + 1, 1, RG_S if t > 0 else 0)
             zf_alloc(t + 1)
             for c in range(4):
                 zf_bank(t + 1, c, "s")
-            if t == 0:
-                w_tr()
             z3_quant(t, 0, 4)
-            zm_quant(t + 1)
+            if not last:
+                zm_quant(t + 1)
+            if t == 0:
+                y_plus_b(2)
+                y_plus_b(3)
+            taps(t + 2, 0, 4)
+            taps(t + 2, 4, 8)
+            if t + 2 < T_Z3:
+                zm_alloc(t + 2)
+                rg_s(t + 2, 1, RG_S)
+            finish(t + 2, 0, 4)
+            if last:
+                zf_quant(5)
+            finish(t + 2, 4, 8)
+            store(t + 2, 0, 1024)
+            if not last:
+                zf_quant(t + 1)
             for tau in yb_plan[t]:
                 y_plus_b(tau)
                 if tau < 2:
                     store(tau, 0, 1024)
-            if t == 0:
-                w_quant()
             for r in range(4, 8):
                 z3_bank(t, r, "s")
-            if t + 2 < T_Z3:
-                zm_alloc(t + 2)
-                rg_s(t + 2, 1, RG_S)
-            zf_quant(t + 1)
-            taps(t + 2, 0, 4, obp, "ob")
-            taps(t + 2, 4, 8, obp, "ob")
-
-        z3_quant(3, 4, 8)
-        finish(5, 0, 4)
-        finish(5, 4, 8)
-        store(5, 0, 1024)
-        z3_alloc(4)
-        zf_alloc(5)
-        for c in range(4):
-            zf_bank(5, c, "s")
-        for r in range(4):
-            z3_bank(4, r, "s")
-        zf_quant(5)
-        z3_quant(4, 0, 4)
-        z3_bank(4, 4, "s")
-        z3_bank(4, 5, "s")
-        taps(6, 0, 4, obp, "ob")
-        z3_bank(4, 6, "s")
-        taps(6, 4, 8, obp, "ob")
-        z3_bank(4, 7, "s")
+        taps(7, 0, 4)
         z3_quant(4, 4, 6)
-        finish(6, 0, 4)
-        taps(7, 0, 4, tpp, "tp")
+        taps(7, 4, 6)
         z3_quant(4, 6, 7)
-        finish(6, 4, 8)
-        store(6, 0, 1024)
-        taps(7, 4, 6, tpp, "tp")
+        taps(7, 6, 7)
         z3_quant(4, 7, 8)
-        taps(7, 6, 7, tpp, "tp")
+        taps(7, 7, 8)
         finish(7, 0, 4)
-        taps(7, 7, 8, obp, "ob")
         finish(7, 4, 6)
         store(7, 0, 768)
         finish(7, 6, 7)

@@ -23,7 +23,7 @@ F_OUT = 128
 FLOPS = 2 * (T_Z3 * NODES * NODES * F_IN + (T_Z2 + T_Z3) * NODES * F_IN * F_OUT)
 
 MANUAL = True
-RG_S = 320
+RG_S = 352
 
 
 def tile_stgnnlayer_pb_t_kernel(tc, z2, S, w2, w3, y01, b, out):
@@ -71,9 +71,8 @@ def tile_stgnnlayer_pb_t_kernel(tc, z2, S, w2, w3, y01, b, out):
         nc.sync.dma_start(out=brow[0:1, :], in_=b.unsqueeze(0))
         for k in range(4):
             nc.sync.dma_start(out=sr[:, 2 * k : 2 * k + 2, :], in_=s_view[:, 2 * k : 2 * k + 2, :])
-            if k == 1:
-                nc.sync.dma_start(out=w2sb[:], in_=w2)
-                nc.sync.dma_start(out=w3sb[:], in_=w3)
+        nc.sync.dma_start(out=w2sb[:], in_=w2)
+        nc.sync.dma_start(out=w3sb[:], in_=w3)
         load_z(1, 0, 4)
         nc.sync.dma_start(out=y01sb[:, 2:4, :], in_=y_view[:, 2:4, :])
         load_z(2, 0, 4)
@@ -297,11 +296,10 @@ def tile_stgnnlayer_pb_t_kernel(tc, z2, S, w2, w3, y01, b, out):
             s_quant(k)
             if k == 1:
                 zf_quant(0)
-            if k == 2:
-                w_tr()
-                w_quant()
+        w_tr()
+        w_quant()
 
-        yb_plan = {0: (), 1: (4, 5), 2: (6, 0), 3: (7, 1), 4: ()}
+        yb_plan = {0: (3,), 1: (4, 0), 2: (5, 1), 3: (6,)}
         for t in range(T_Z3):
             last = t == T_Z3 - 1
             if t > 0:
@@ -315,28 +313,27 @@ def tile_stgnnlayer_pb_t_kernel(tc, z2, S, w2, w3, y01, b, out):
             zf_alloc(t + 1)
             for c in range(4):
                 zf_bank(t + 1, c, "s")
+            if last:
+                y_plus_b(7)
             z3_quant(t, 0, 4)
             if not last:
                 zm_quant(t + 1)
             if t == 0:
                 y_plus_b(2)
-                y_plus_b(3)
             taps(t + 2, 0, 4)
             taps(t + 2, 4, 8)
             if t + 2 < T_Z3:
                 zm_alloc(t + 2)
                 rg_s(t + 2, 1, RG_S)
             finish(t + 2, 0, 4)
-            if last:
-                zf_quant(5)
             finish(t + 2, 4, 8)
             store(t + 2, 0, 1024)
+            zf_quant(t + 1)
             if not last:
-                zf_quant(t + 1)
-            for tau in yb_plan[t]:
-                y_plus_b(tau)
-                if tau < 2:
-                    store(tau, 0, 1024)
+                for tau in yb_plan[t]:
+                    y_plus_b(tau)
+                    if tau < 2:
+                        store(tau, 0, 1024)
             for r in range(4, 8):
                 z3_bank(t, r, "s")
         taps(7, 0, 4)

@@ -1,8 +1,6 @@
 from contextlib import ExitStack
 
-import concourse.bass as bass
 import concourse.mybir as mybir
-import concourse.tile as tile
 from concourse.masks import make_identity
 
 F32 = mybir.dt.float32
@@ -19,333 +17,349 @@ T_Z3 = 5
 NODES = 1024
 F_IN = 512
 F_OUT = 128
+TILES = NODES // P
+BANK = 512
 
 FLOPS = 2 * (T_Z3 * NODES * NODES * F_IN + (T_Z2 + T_Z3) * NODES * F_IN * F_OUT)
 
-MANUAL = True
-RG_S = 352
+SCALAR_REGROUP_COLUMNS = 352
+
+BIAS_ADDS_AFTER_ROUND = {0: (3,), 1: (4, 0), 2: (5, 1), 3: (6,)}
 
 
 def tile_stgnnlayer_pb_t_kernel(tc, z2, S, w2, w3, y01, b, out):
     nc = tc.nc
     with ExitStack() as ctx:
-        const = ctx.enter_context(tc.tile_pool(name="const", bufs=1))
-        rot2 = ctx.enter_context(tc.tile_pool(name="rot2", bufs=2))
-        rot3 = ctx.enter_context(tc.tile_pool(name="rot3", bufs=3))
-        psp = ctx.enter_context(tc.psum_pool(name="psp", bufs=8))
-        if MANUAL:
-            ctx.enter_context(tc.manual_schedule())
+        keep = ctx.enter_context(tc.tile_pool(name="keep", bufs=1))
+        two = ctx.enter_context(tc.tile_pool(name="two", bufs=2))
+        three = ctx.enter_context(tc.tile_pool(name="three", bufs=3))
+        psum = ctx.enter_context(tc.psum_pool(name="psum", bufs=8))
+        ctx.enter_context(tc.manual_schedule())
 
-        brow = const.tile([P, F_OUT], BF16, name="brow")
-        ones = const.tile([P, P], BF16, name="ones")
-        nc.vector.memset(brow[:], 0.0)
+        bias_row = keep.tile([P, F_OUT], BF16, name="bias_row")
+        ones = keep.tile([P, P], BF16, name="ones")
+        nc.vector.memset(bias_row[:], 0.0)
         nc.vector.memset(ones[:], 1.0)
-        ident_f = const.tile([P, P], F32, name="ident_f")
-        make_identity(nc, ident_f[:])
-        perm_f = const.tile([P, P], F32, name="perm_f")
+        ident_f32 = keep.tile([P, P], F32, name="ident_f32")
+        make_identity(nc, ident_f32[:])
+        sort_f32 = keep.tile([P, P], F32, name="sort_f32")
         nc.vector.tensor_copy(
-            out=perm_f[:].rearrange("p (s a) -> p s a", s=4),
-            in_=ident_f[:].rearrange("p (a s) -> p s a", s=4),
+            out=sort_f32[:].rearrange("p (s a) -> p s a", s=4),
+            in_=ident_f32[:].rearrange("p (a s) -> p s a", s=4),
         )
-        ident_b = const.tile([P, P], BF16, name="ident_b")
-        nc.vector.tensor_copy(out=ident_b[:], in_=ident_f[:])
+        ident_bf16 = keep.tile([P, P], BF16, name="ident_bf16")
+        nc.vector.tensor_copy(out=ident_bf16[:], in_=ident_f32[:])
 
-        zr = [const.tile([P, 8, F_IN], BF16, name="zr%d" % t) for t in range(T_Z2)]
-        sr = const.tile([P, 8, NODES], BF16, name="sr")
-        y01sb = const.tile([P, T_OUT, 8 * F_OUT], BF16, name="y01sb")
-        yb = const.tile([P, T_OUT, 8 * F_OUT], F32, name="yb")
-        w2sb = const.tile([P, F_IN], BF16, name="w2sb")
-        w3sb = const.tile([P, F_IN], BF16, name="w3sb")
-        bb = const.tile([P, F_OUT], F32, name="bb")
+        z2_rows = [keep.tile([P, 8, F_IN], BF16, name="z2_rows%d" % t) for t in range(T_Z2)]
+        s_rows = keep.tile([P, TILES, NODES], BF16, name="s_rows")
+        y01_rows = keep.tile([P, T_OUT, TILES * F_OUT], BF16, name="y01_rows")
+        y_rows = keep.tile([P, T_OUT, TILES * F_OUT], F32, name="y_rows")
+        w2_rows = keep.tile([P, F_IN], BF16, name="w2_rows")
+        w3_rows = keep.tile([P, F_IN], BF16, name="w3_rows")
+        bias_all = keep.tile([P, F_OUT], F32, name="bias_all")
 
-        def load_z(t, c_lo, c_hi):
+        def load_z2(t, c_lo, c_hi):
             src = z2[0, t].rearrange("(c p e) f -> p c e f", c=4, p=P, e=2)
-            dst = zr[t][:].rearrange("p (c e) f -> p c e f", e=2)
+            dst = z2_rows[t][:].rearrange("p (c e) f -> p c e f", e=2)
             nc.sync.dma_start(out=dst[:, c_lo:c_hi], in_=src[:, c_lo:c_hi])
 
-        s_view = S.rearrange("(q r) m -> q r m", r=8)
-        y_view = y01[0].rearrange("t (q r) o -> q t (r o)", r=8)
+        s_view = S.rearrange("(q r) m -> q r m", r=TILES)
+        y01_view = y01[0].rearrange("t (q r) o -> q t (r o)", r=TILES)
 
         for c in range(4):
-            load_z(0, c, c + 1)
-        nc.sync.dma_start(out=brow[0:1, :], in_=b.unsqueeze(0))
+            load_z2(0, c, c + 1)
+        nc.sync.dma_start(out=bias_row[0:1, :], in_=b.unsqueeze(0))
         for k in range(4):
-            nc.sync.dma_start(out=sr[:, 2 * k : 2 * k + 2, :], in_=s_view[:, 2 * k : 2 * k + 2, :])
-        nc.sync.dma_start(out=w2sb[:], in_=w2)
-        nc.sync.dma_start(out=w3sb[:], in_=w3)
-        load_z(1, 0, 4)
-        nc.sync.dma_start(out=y01sb[:, 2:4, :], in_=y_view[:, 2:4, :])
-        load_z(2, 0, 4)
-        nc.sync.dma_start(out=y01sb[:, 4:8, :], in_=y_view[:, 4:8, :])
-        load_z(3, 0, 4)
-        nc.sync.dma_start(out=y01sb[:, 0:2, :], in_=y_view[:, 0:2, :])
-        load_z(4, 0, 4)
-        load_z(5, 0, 4)
+            nc.sync.dma_start(out=s_rows[:, 2 * k : 2 * k + 2, :], in_=s_view[:, 2 * k : 2 * k + 2, :])
+        nc.sync.dma_start(out=w2_rows[:], in_=w2)
+        nc.sync.dma_start(out=w3_rows[:], in_=w3)
+        load_z2(1, 0, 4)
+        nc.sync.dma_start(out=y01_rows[:, 2:4, :], in_=y01_view[:, 2:4, :])
+        load_z2(2, 0, 4)
+        nc.sync.dma_start(out=y01_rows[:, 4:8, :], in_=y01_view[:, 4:8, :])
+        load_z2(3, 0, 4)
+        nc.sync.dma_start(out=y01_rows[:, 0:2, :], in_=y01_view[:, 0:2, :])
+        load_z2(4, 0, 4)
+        load_z2(5, 0, 4)
 
-        sqc = const.tile([P, 2048], U32, name="sqc", align_bytes=64)
-        sqs = const.tile([P, 2048], U8, name="sqs", align_bytes=64)
-        w2c = const.tile([P, P], U32, name="w2c", align_bytes=64)
-        w2s = const.tile([P, P], U8, name="w2s", align_bytes=64)
-        w3c = const.tile([P, P], U32, name="w3c", align_bytes=64)
-        w3s = const.tile([P, P], U8, name="w3s", align_bytes=64)
-        gm = {}
-        zmc = {}
-        zms = {}
-        gf = {}
-        zfc = {}
-        zfs = {}
-        g3 = {}
-        z3c = {}
-        z3s = {}
-        obs = {}
+        s_codes = keep.tile([P, 2048], U32, name="s_codes", align_bytes=64)
+        s_scales = keep.tile([P, 2048], U8, name="s_scales", align_bytes=64)
+        w2_codes = keep.tile([P, P], U32, name="w2_codes", align_bytes=64)
+        w2_scales = keep.tile([P, P], U8, name="w2_scales", align_bytes=64)
+        w3_codes = keep.tile([P, P], U32, name="w3_codes", align_bytes=64)
+        w3_scales = keep.tile([P, P], U8, name="w3_scales", align_bytes=64)
+        s_grouped = {}
+        zn_grouped, zn_codes, zn_scales = {}, {}, {}
+        zf_grouped, zf_codes, zf_scales = {}, {}, {}
+        z3_grouped, z3_codes, z3_scales = {}, {}, {}
+        tap_banks = {}
 
-        def evac(eng, dst, src):
-            if eng == "s":
-                nc.scalar.copy(out=dst, in_=src)
-            else:
-                nc.vector.tensor_copy(out=dst, in_=src)
+        s_words = s_rows[:].bitcast(F32)
 
-        srw = sr[:].bitcast(F32)
-
-        gs_tiles = {}
-
-        def s_bank(k, g, eng):
+        def transpose_s(k, g):
             if g == 0:
-                gs_tiles[k] = rot2.tile([P, 2048], BF16, tag="gs", name="gs%d" % k, align_bytes=64)
-            gsw = gs_tiles[k][:].bitcast(F32)
-            tb = psp.tile([P, 512], F32, tag="ps", name="tbs%d_%d" % (k, g))
+                s_grouped[k] = two.tile([P, 2048], BF16, tag="s_grouped", name="s_grouped%d" % k, align_bytes=64)
+            bank = psum.tile([P, BANK], F32, tag="bank", name="s_bank%d_%d" % (k, g))
             for u in range(2):
-                for r2 in range(2):
+                for i in range(2):
                     nc.tensor.transpose(
-                        tb[:, u * 256 + r2 * 128 : u * 256 + r2 * 128 + 128],
-                        srw[:, 2 * k + r2, (2 * g + u) * 128 : (2 * g + u) * 128 + 128],
-                        ident_f[:],
+                        bank[:, u * 256 + i * 128 : u * 256 + i * 128 + 128],
+                        s_words[:, 2 * k + i, (2 * g + u) * 128 : (2 * g + u) * 128 + 128],
+                        ident_f32[:],
                     )
-            evac(
-                eng,
-                gsw[:, g * 512 : (g + 1) * 512].rearrange("p (n u) -> p n u", u=2),
-                tb[:].rearrange("p (u n) -> p n u", u=2),
+            nc.scalar.copy(
+                out=s_grouped[k][:].bitcast(F32)[:, g * 512 : (g + 1) * 512].rearrange("p (n u) -> p n u", u=2),
+                in_=bank[:].rearrange("p (u n) -> p n u", u=2),
             )
 
-        def s_quant(k):
-            gs = gs_tiles[k]
+        def quantise_s(k):
             nc.vector.quantize_mx(
-                out=sqc[:, k * 512 : (k + 1) * 512].bitcast(FP8X4),
-                scales=sqs[:, k * 512 : (k + 1) * 512],
-                in_=gs[:],
+                out=s_codes[:, k * 512 : (k + 1) * 512].bitcast(FP8X4),
+                scales=s_scales[:, k * 512 : (k + 1) * 512],
+                in_=s_grouped[k][:],
             )
 
-        gw2 = const.tile([P, F_IN], BF16, name="gw2", align_bytes=64)
-        gw3 = const.tile([P, F_IN], BF16, name="gw3", align_bytes=64)
+        w2_grouped = keep.tile([P, F_IN], BF16, name="w2_grouped", align_bytes=64)
+        w3_grouped = keep.tile([P, F_IN], BF16, name="w3_grouped", align_bytes=64)
 
-        def w_tr():
-            tb2 = psp.tile([P, 256], F32, tag="ps", name="tbw2")
-            w2w = w2sb[:].bitcast(F32)
+        def transpose_w():
+            w2_bank = psum.tile([P, 256], F32, tag="bank", name="w2_bank")
+            w2_words = w2_rows[:].bitcast(F32)
             for u in range(2):
-                nc.tensor.transpose(tb2[:, u * 128 : u * 128 + 128], w2w[:, u * 128 : u * 128 + 128], ident_f[:])
-            evac("s", gw2[:].bitcast(F32).rearrange("p (o u) -> p o u", u=2), tb2[:].rearrange("p (u o) -> p o u", u=2))
-            tb3 = psp.tile([P, 512], BF16, tag="ps", name="tbw3")
+                nc.tensor.transpose(
+                    w2_bank[:, u * 128 : u * 128 + 128], w2_words[:, u * 128 : u * 128 + 128], ident_f32[:]
+                )
+            nc.scalar.copy(
+                out=w2_grouped[:].bitcast(F32).rearrange("p (o u) -> p o u", u=2),
+                in_=w2_bank[:].rearrange("p (u o) -> p o u", u=2),
+            )
+            w3_bank = psum.tile([P, 512], BF16, tag="bank", name="w3_bank")
             for j in range(4):
-                nc.tensor.transpose(tb3[:, j * 128 : j * 128 + 128], w3sb[:, j * 128 : j * 128 + 128], ident_b[:])
-            evac("s", gw3[:].rearrange("p (o j) -> p o j", j=4), tb3[:].rearrange("p (j o) -> p o j", j=4))
+                nc.tensor.transpose(
+                    w3_bank[:, j * 128 : j * 128 + 128], w3_rows[:, j * 128 : j * 128 + 128], ident_bf16[:]
+                )
+            nc.scalar.copy(
+                out=w3_grouped[:].rearrange("p (o j) -> p o j", j=4),
+                in_=w3_bank[:].rearrange("p (j o) -> p o j", j=4),
+            )
 
-        def w_quant():
-            nc.vector.quantize_mx(out=w2c[:].bitcast(FP8X4), scales=w2s[:], in_=gw2[:])
-            nc.vector.quantize_mx(out=w3c[:].bitcast(FP8X4), scales=w3s[:], in_=gw3[:])
+        def quantise_w():
+            nc.vector.quantize_mx(out=w2_codes[:].bitcast(FP8X4), scales=w2_scales[:], in_=w2_grouped[:])
+            nc.vector.quantize_mx(out=w3_codes[:].bitcast(FP8X4), scales=w3_scales[:], in_=w3_grouped[:])
 
-        def bias_spread():
-            pb = psp.tile([P, F_OUT], F32, tag="ps", name="pb")
-            nc.tensor.matmul(out=pb[:], lhsT=ones[:], rhs=brow[:], start=True, stop=True)
-            evac("s", bb[:], pb[:])
+        def spread_bias():
+            bias_bank = psum.tile([P, F_OUT], F32, tag="bank", name="bias_bank")
+            nc.tensor.matmul(out=bias_bank[:], lhsT=ones[:], rhs=bias_row[:], start=True, stop=True)
+            nc.scalar.copy(out=bias_all[:], in_=bias_bank[:])
 
-        def zf_alloc(t):
-            gf[t] = rot2.tile([P, 4096], BF16, tag="gf", name="gf%d" % t, align_bytes=64)
-            zfc[t] = rot3.tile([P, 1024], U32, tag="zfc", name="zfc%d" % t, align_bytes=64)
-            zfs[t] = rot3.tile([P, 1024], U8, tag="zfs", name="zfs%d" % t, align_bytes=64)
+        def new_zf(t):
+            zf_grouped[t] = two.tile([P, 4096], BF16, tag="zf_grouped", name="zf_grouped%d" % t, align_bytes=64)
+            zf_codes[t] = three.tile([P, 1024], U32, tag="zf_codes", name="zf_codes%d" % t, align_bytes=64)
+            zf_scales[t] = three.tile([P, 1024], U8, tag="zf_scales", name="zf_scales%d" % t, align_bytes=64)
 
-        def zf_bank(t, c, eng):
-            zw = zr[t][:].bitcast(F32)
-            tb = psp.tile([P, 512], F32, tag="ps", name="tbz%d_%d" % (t, c))
+        def transpose_z2(t, c):
+            z2_words = z2_rows[t][:].bitcast(F32)
+            bank = psum.tile([P, BANK], F32, tag="bank", name="zf_bank%d_%d" % (t, c))
             for u in range(2):
                 for e in range(2):
                     nc.tensor.transpose(
-                        tb[:, u * 256 + e * 128 : u * 256 + e * 128 + 128],
-                        zw[:, 2 * c + e, u * 128 : u * 128 + 128],
-                        perm_f[:],
+                        bank[:, u * 256 + e * 128 : u * 256 + e * 128 + 128],
+                        z2_words[:, 2 * c + e, u * 128 : u * 128 + 128],
+                        sort_f32[:],
                     )
-            gfw = gf[t][:].bitcast(F32).rearrange("p (r q u) -> p r q u", r=8, q=128, u=2)
-            evac(eng, gfw[:, :, 32 * c : 32 * c + 32, :], tb[:].rearrange("p (u r q) -> p r q u", u=2, r=8, q=32))
-
-        def zf_quant(t):
-            nc.vector.quantize_mx(out=zfc[t][:].bitcast(FP8X4), scales=zfs[t][:], in_=gf[t][:])
-
-        def zm_alloc(t):
-            gm[t] = rot2.tile([P, 2, 2048], BF16, tag="gm", name="gm%d" % t, align_bytes=64)
-            zmc[t] = rot2.tile([P, 1024], U32, tag="zmc", name="zmc%d" % t, align_bytes=64)
-            zms[t] = rot2.tile([P, 1024], U8, tag="zms", name="zms%d" % t, align_bytes=64)
-
-        def zm_views(t, g):
-            dst = gm[t][:, g, :].rearrange("p (c i j) -> p c j i", i=4, j=4)
-            src = zr[t][:, 4 * g : 4 * g + 4, :].rearrange("p j (c i) -> p c j i", i=4)
-            return dst, src
-
-        def rg_v(t, g, xs):
-            dst, src = zm_views(t, g)
-            cv = (F_IN - xs) // 4
-            nc.vector.tensor_copy(out=dst[:, 0:cv], in_=src[:, 0:cv])
-
-        def rg_s(t, g, xs):
-            dst, src = zm_views(t, g)
-            cv = (F_IN - xs) // 4
-            nc.scalar.copy(out=dst[:, cv:128], in_=src[:, cv:128])
-
-        def zm_quant(t):
-            nc.vector.quantize_mx(
-                out=zmc[t][:].bitcast(FP8X4), scales=zms[t][:], in_=gm[t][:].rearrange("p g x -> p (g x)")
+            grouped_words = zf_grouped[t][:].bitcast(F32).rearrange("p (r q u) -> p r q u", r=8, q=128, u=2)
+            nc.scalar.copy(
+                out=grouped_words[:, :, 32 * c : 32 * c + 32, :],
+                in_=bank[:].rearrange("p (u r q) -> p r q u", u=2, r=8, q=32),
             )
 
-        def z3_alloc(t):
-            g3[t] = rot2.tile([P, 8, 512], BF16, tag="g3", name="g3_%d" % t, align_bytes=64)
-            z3c[t] = rot2.tile([P, 1024], U32, tag="z3c", name="z3c%d" % t, align_bytes=64)
-            z3s[t] = rot2.tile([P, 1024], U8, tag="z3s", name="z3s%d" % t, align_bytes=64)
+        def quantise_zf(t):
+            nc.vector.quantize_mx(out=zf_codes[t][:].bitcast(FP8X4), scales=zf_scales[t][:], in_=zf_grouped[t][:])
 
-        def z3_bank(t, r, eng):
-            zb = psp.tile([P, 512], F32, tag="ps", name="zb%d_%d" % (t, r))
-            k, r2 = divmod(r, 2)
+        def new_zn(t):
+            zn_grouped[t] = two.tile([P, 2, 2048], BF16, tag="zn_grouped", name="zn_grouped%d" % t, align_bytes=64)
+            zn_codes[t] = two.tile([P, 1024], U32, tag="zn_codes", name="zn_codes%d" % t, align_bytes=64)
+            zn_scales[t] = two.tile([P, 1024], U8, tag="zn_scales", name="zn_scales%d" % t, align_bytes=64)
+
+        def regroup_views(t, g):
+            dst = zn_grouped[t][:, g, :].rearrange("p (c i j) -> p c j i", i=4, j=4)
+            src = z2_rows[t][:, 4 * g : 4 * g + 4, :].rearrange("p j (c i) -> p c j i", i=4)
+            return dst, src
+
+        def regroup_on_vector(t, g, scalar_columns):
+            dst, src = regroup_views(t, g)
+            split = (F_IN - scalar_columns) // 4
+            nc.vector.tensor_copy(out=dst[:, 0:split], in_=src[:, 0:split])
+
+        def regroup_on_scalar(t, g, scalar_columns):
+            dst, src = regroup_views(t, g)
+            split = (F_IN - scalar_columns) // 4
+            nc.scalar.copy(out=dst[:, split:128], in_=src[:, split:128])
+
+        def quantise_zn(t):
+            nc.vector.quantize_mx(
+                out=zn_codes[t][:].bitcast(FP8X4),
+                scales=zn_scales[t][:],
+                in_=zn_grouped[t][:].rearrange("p g x -> p (g x)"),
+            )
+
+        def new_z3(t):
+            z3_grouped[t] = two.tile([P, TILES, 512], BF16, tag="z3_grouped", name="z3_grouped%d" % t, align_bytes=64)
+            z3_codes[t] = two.tile([P, 1024], U32, tag="z3_codes", name="z3_codes%d" % t, align_bytes=64)
+            z3_scales[t] = two.tile([P, 1024], U8, tag="z3_scales", name="z3_scales%d" % t, align_bytes=64)
+
+        def shift(t, r):
+            bank = psum.tile([P, BANK], F32, tag="bank", name="z3_bank%d_%d" % (t, r))
+            k, i = divmod(r, 2)
             for j in range(4):
                 for g in range(2):
-                    a0 = g * 512 + j * 128
-                    b0 = k * 512 + g * 256 + r2 * 128
+                    z_col = g * 512 + j * 128
+                    s_col = k * 512 + g * 256 + i * 128
                     nc.tensor.matmul_mx(
-                        out=zb[:, j * 128 : j * 128 + 128],
-                        lhsT=zmc[t][:, a0 : a0 + 128].bitcast(FP8X4),
-                        lhsT_scale=zms[t][:, a0 : a0 + 128],
-                        rhs=sqc[:, b0 : b0 + 128].bitcast(FP8X4),
-                        rhs_scale=sqs[:, b0 : b0 + 128],
+                        out=bank[:, j * 128 : j * 128 + 128],
+                        lhsT=zn_codes[t][:, z_col : z_col + 128].bitcast(FP8X4),
+                        lhsT_scale=zn_scales[t][:, z_col : z_col + 128],
+                        rhs=s_codes[:, s_col : s_col + 128].bitcast(FP8X4),
+                        rhs_scale=s_scales[:, s_col : s_col + 128],
                         start=(g == 0),
                         stop=(g == 1),
                     )
-            evac(eng, g3[t][:, r, :].rearrange("p (q j) -> p q j", j=4), zb[:].rearrange("p (j q) -> p q j", j=4))
-
-        def z3_quant(t, r_lo, r_hi):
-            nc.vector.quantize_mx(
-                out=z3c[t][:, r_lo * 128 : r_hi * 128].bitcast(FP8X4),
-                scales=z3s[t][:, r_lo * 128 : r_hi * 128],
-                in_=g3[t][:, r_lo:r_hi, :].rearrange("p r x -> p (r x)"),
+            nc.scalar.copy(
+                out=z3_grouped[t][:, r, :].rearrange("p (q j) -> p q j", j=4),
+                in_=bank[:].rearrange("p (j q) -> p q j", j=4),
             )
 
-        def taps(tau, r_lo, r_hi):
-            ob = psp.tile([P, (r_hi - r_lo) * 128], F32, tag="ps", name="ob%d_%d" % (tau, r_lo))
-            obs[(tau, r_lo)] = ob
+        def quantise_z3(t, r_lo, r_hi):
+            nc.vector.quantize_mx(
+                out=z3_codes[t][:, r_lo * 128 : r_hi * 128].bitcast(FP8X4),
+                scales=z3_scales[t][:, r_lo * 128 : r_hi * 128],
+                in_=z3_grouped[t][:, r_lo:r_hi, :].rearrange("p r x -> p (r x)"),
+            )
+
+        def taps(t_out, r_lo, r_hi):
+            bank = psum.tile([P, (r_hi - r_lo) * 128], F32, tag="bank", name="tap_bank%d_%d" % (t_out, r_lo))
+            tap_banks[(t_out, r_lo)] = bank
             for r in range(r_lo, r_hi):
-                i = r - r_lo
-                rp = (r % 2) * 4 + r // 2
+                col = (r - r_lo) * 128
+                zf_col = ((r % 2) * 4 + r // 2) * 128
                 nc.tensor.matmul_mx(
-                    out=ob[:, i * 128 : i * 128 + 128],
-                    lhsT=zfc[tau - 2][:, rp * 128 : rp * 128 + 128].bitcast(FP8X4),
-                    lhsT_scale=zfs[tau - 2][:, rp * 128 : rp * 128 + 128],
-                    rhs=w2c[:].bitcast(FP8X4),
-                    rhs_scale=w2s[:],
+                    out=bank[:, col : col + 128],
+                    lhsT=zf_codes[t_out - 2][:, zf_col : zf_col + 128].bitcast(FP8X4),
+                    lhsT_scale=zf_scales[t_out - 2][:, zf_col : zf_col + 128],
+                    rhs=w2_codes[:].bitcast(FP8X4),
+                    rhs_scale=w2_scales[:],
                     start=True,
-                    stop=(tau < 3),
+                    stop=(t_out < 3),
                 )
-                if tau >= 3:
+                if t_out >= 3:
                     nc.tensor.matmul_mx(
-                        out=ob[:, i * 128 : i * 128 + 128],
-                        lhsT=z3c[tau - 3][:, r * 128 : r * 128 + 128].bitcast(FP8X4),
-                        lhsT_scale=z3s[tau - 3][:, r * 128 : r * 128 + 128],
-                        rhs=w3c[:].bitcast(FP8X4),
-                        rhs_scale=w3s[:],
+                        out=bank[:, col : col + 128],
+                        lhsT=z3_codes[t_out - 3][:, r * 128 : r * 128 + 128].bitcast(FP8X4),
+                        lhsT_scale=z3_scales[t_out - 3][:, r * 128 : r * 128 + 128],
+                        rhs=w3_codes[:].bitcast(FP8X4),
+                        rhs_scale=w3_scales[:],
                         start=False,
                         stop=True,
                     )
 
-        def y_plus_b(tau):
+        def add_bias(t_out):
             nc.vector.tensor_tensor(
-                out=yb[:, tau, :].rearrange("p (r o) -> p r o", o=F_OUT),
-                in0=y01sb[:, tau, :].rearrange("p (r o) -> p r o", o=F_OUT),
-                in1=bb[:].unsqueeze(1).to_broadcast([P, 8, F_OUT]),
+                out=y_rows[:, t_out, :].rearrange("p (r o) -> p r o", o=F_OUT),
+                in0=y01_rows[:, t_out, :].rearrange("p (r o) -> p r o", o=F_OUT),
+                in1=bias_all[:].unsqueeze(1).to_broadcast([P, TILES, F_OUT]),
                 op=ADD,
             )
 
-        def finish(tau, r_lo, r_hi):
+        def add_taps(t_out, r_lo, r_hi):
             nc.vector.tensor_tensor(
-                out=yb[:, tau, r_lo * 128 : r_hi * 128],
-                in0=obs[(tau, r_lo)][:],
-                in1=yb[:, tau, r_lo * 128 : r_hi * 128],
+                out=y_rows[:, t_out, r_lo * 128 : r_hi * 128],
+                in0=tap_banks[(t_out, r_lo)][:],
+                in1=y_rows[:, t_out, r_lo * 128 : r_hi * 128],
                 op=ADD,
             )
 
-        def store(tau, lo, hi):
-            o_view = out[0, tau].rearrange("(q r) o -> q (r o)", r=8)
-            nc.sync.dma_start(out=o_view[:, lo:hi], in_=yb[:, tau, lo:hi])
+        def store(t_out, r_lo, r_hi):
+            y_view = out[0, t_out].rearrange("(q r) o -> q (r o)", r=TILES)
+            nc.sync.dma_start(out=y_view[:, r_lo * 128 : r_hi * 128], in_=y_rows[:, t_out, r_lo * 128 : r_hi * 128])
 
-        zf_alloc(0)
-        zm_alloc(0)
+        new_zf(0)
+        new_zn(0)
         for c in range(4):
-            zf_bank(0, c, "s")
-        bias_spread()
-        rg_v(0, 0, 0)
-        rg_v(0, 1, 0)
-        zm_quant(0)
-        zm_alloc(1)
-        z3_alloc(0)
+            transpose_z2(0, c)
+        spread_bias()
+        regroup_on_vector(0, 0, 0)
+        regroup_on_vector(0, 1, 0)
+        quantise_zn(0)
+        new_zn(1)
+        new_z3(0)
         for k in range(4):
-            s_bank(k, 0, "s")
-            s_bank(k, 1, "s")
-            s_quant(k)
+            transpose_s(k, 0)
+            transpose_s(k, 1)
+            quantise_s(k)
             if k == 1:
-                zf_quant(0)
-        w_tr()
-        w_quant()
+                quantise_zf(0)
+        transpose_w()
+        quantise_w()
 
-        yb_plan = {0: (3,), 1: (4, 0), 2: (5, 1), 3: (6,)}
-        for t in range(T_Z3):
-            last = t == T_Z3 - 1
+        for t in range(T_Z3 - 1):
             if t > 0:
-                z3_quant(t - 1, 4, 8)
-                z3_alloc(t)
+                quantise_z3(t - 1, 4, 8)
+                new_z3(t)
             for r in range(4):
-                z3_bank(t, r, "s")
-            if not last:
-                rg_v(t + 1, 0, 0)
-                rg_v(t + 1, 1, RG_S if t > 0 else 0)
-            zf_alloc(t + 1)
+                shift(t, r)
+            regroup_on_vector(t + 1, 0, 0)
+            regroup_on_vector(t + 1, 1, SCALAR_REGROUP_COLUMNS if t > 0 else 0)
+            new_zf(t + 1)
             for c in range(4):
-                zf_bank(t + 1, c, "s")
-            if last:
-                y_plus_b(7)
-            z3_quant(t, 0, 4)
-            if not last:
-                zm_quant(t + 1)
+                transpose_z2(t + 1, c)
+            quantise_z3(t, 0, 4)
+            quantise_zn(t + 1)
             if t == 0:
-                y_plus_b(2)
+                add_bias(2)
             taps(t + 2, 0, 4)
             taps(t + 2, 4, 8)
             if t + 2 < T_Z3:
-                zm_alloc(t + 2)
-                rg_s(t + 2, 1, RG_S)
-            finish(t + 2, 0, 4)
-            finish(t + 2, 4, 8)
-            store(t + 2, 0, 1024)
-            zf_quant(t + 1)
-            if not last:
-                for tau in yb_plan[t]:
-                    y_plus_b(tau)
-                    if tau < 2:
-                        store(tau, 0, 1024)
+                new_zn(t + 2)
+                regroup_on_scalar(t + 2, 1, SCALAR_REGROUP_COLUMNS)
+            add_taps(t + 2, 0, 4)
+            add_taps(t + 2, 4, 8)
+            store(t + 2, 0, 8)
+            quantise_zf(t + 1)
+            for t_out in BIAS_ADDS_AFTER_ROUND[t]:
+                add_bias(t_out)
+                if t_out < 2:
+                    store(t_out, 0, 8)
             for r in range(4, 8):
-                z3_bank(t, r, "s")
+                shift(t, r)
+
+        new_z3(4)
+        new_zf(5)
+        for c in range(4):
+            transpose_z2(5, c)
+        quantise_z3(3, 4, 8)
+        for r in range(4):
+            shift(4, r)
+        taps(6, 0, 4)
+        taps(6, 4, 8)
+        for r in range(4, 8):
+            shift(4, r)
+        add_bias(7)
+        quantise_zf(5)
+        add_taps(6, 0, 4)
+        add_taps(6, 4, 8)
+        store(6, 0, 8)
+        quantise_z3(4, 0, 4)
         taps(7, 0, 4)
-        z3_quant(4, 4, 6)
+        quantise_z3(4, 4, 6)
         taps(7, 4, 6)
-        z3_quant(4, 6, 7)
+        quantise_z3(4, 6, 7)
         taps(7, 6, 7)
-        z3_quant(4, 7, 8)
+        quantise_z3(4, 7, 8)
         taps(7, 7, 8)
-        finish(7, 0, 4)
-        finish(7, 4, 6)
-        store(7, 0, 768)
-        finish(7, 6, 7)
-        finish(7, 7, 8)
-        store(7, 768, 1024)
+        add_taps(7, 0, 4)
+        store(7, 0, 4)
+        add_taps(7, 4, 6)
+        store(7, 4, 6)
+        add_taps(7, 6, 7)
+        add_taps(7, 7, 8)
+        store(7, 6, 8)

@@ -98,7 +98,7 @@ def tile_stgnnlayer_pb_t_kernel(tc, z2, S, w2, w3, y01, b, out):
 
         def transpose_s(k, g):
             if g == 0:
-                s_grouped[k] = two.tile([P, 2048], BF16, tag="s_grouped", name="s_grouped%d" % k, align_bytes=64)
+                s_grouped[k] = keep.tile([P, 2048], BF16, name="s_grouped%d" % k, align_bytes=64)
             bank = psum.tile([P, BANK], F32, tag="bank", name="s_bank%d_%d" % (k, g))
             for u in range(2):
                 for i in range(2):
@@ -296,7 +296,7 @@ def tile_stgnnlayer_pb_t_kernel(tc, z2, S, w2, w3, y01, b, out):
             transpose_s(k, 0)
             transpose_s(k, 1)
             quantise_s(k)
-            if k == 1:
+            if k == 0:
                 quantise_zf(0)
         transpose_w()
         quantise_w()
@@ -313,9 +313,9 @@ def tile_stgnnlayer_pb_t_kernel(tc, z2, S, w2, w3, y01, b, out):
             for c in range(4):
                 transpose_z2(t + 1, c)
             quantise_z3(t, 0, 4)
-            quantise_zn(t + 1)
             if t == 0:
                 add_bias(2)
+            quantise_zn(t + 1)
             taps(t + 2, 0, 4)
             taps(t + 2, 4, 8)
             if t + 2 < T_Z3:
@@ -340,20 +340,21 @@ def tile_stgnnlayer_pb_t_kernel(tc, z2, S, w2, w3, y01, b, out):
         for r in range(4):
             shift(4, r)
         taps(6, 0, 4)
-        taps(6, 4, 8)
         for r in range(4, 8):
             shift(4, r)
         add_bias(7)
         quantise_zf(5)
         add_taps(6, 0, 4)
-        add_taps(6, 4, 8)
-        store(6, 0, 8)
+        store(6, 0, 4)
         quantise_z3(4, 0, 4)
+        taps(6, 4, 8)
         taps(7, 0, 4)
         quantise_z3(4, 4, 6)
         taps(7, 4, 6)
         quantise_z3(4, 6, 7)
         taps(7, 6, 7)
+        add_taps(6, 4, 8)
+        store(6, 4, 8)
         quantise_z3(4, 7, 8)
         taps(7, 7, 8)
         add_taps(7, 0, 4)

@@ -22,7 +22,7 @@ BANK = 512
 
 FLOPS = 2 * (T_Z3 * NODES * NODES * F_IN + (T_Z2 + T_Z3) * NODES * F_IN * F_OUT)
 
-SCALAR_REGROUP_COLUMNS = 352
+SCALAR_REGROUP_COLUMNS = 304
 
 BIAS_ADDS_AFTER_ROUND = {0: (3,), 1: (4, 0), 2: (5, 1), 3: (6,)}
 
@@ -70,11 +70,14 @@ def tile_stgnnlayer_pb_t_kernel(tc, z2, S, w2, w3, y01, b, out):
             load_z2(0, c, c + 1)
         nc.sync.dma_start(out=bias_row[0:1, :], in_=b.unsqueeze(0))
         for k in range(4):
+            if k == 3:
+                nc.sync.dma_start(out=y01_rows[:, 2:3, :], in_=y01_view[:, 2:3, :])
             nc.sync.dma_start(out=s_rows[:, 2 * k : 2 * k + 2, :], in_=s_view[:, 2 * k : 2 * k + 2, :])
+        load_z2(1, 0, 2)
+        load_z2(1, 2, 4)
         nc.sync.dma_start(out=w2_rows[:], in_=w2)
         nc.sync.dma_start(out=w3_rows[:], in_=w3)
-        load_z2(1, 0, 4)
-        nc.sync.dma_start(out=y01_rows[:, 2:4, :], in_=y01_view[:, 2:4, :])
+        nc.sync.dma_start(out=y01_rows[:, 3:4, :], in_=y01_view[:, 3:4, :])
         load_z2(2, 0, 4)
         nc.sync.dma_start(out=y01_rows[:, 4:8, :], in_=y01_view[:, 4:8, :])
         load_z2(3, 0, 4)
@@ -295,27 +298,42 @@ def tile_stgnnlayer_pb_t_kernel(tc, z2, S, w2, w3, y01, b, out):
         for k in range(4):
             transpose_s(k, 0)
             transpose_s(k, 1)
+            if k == 3:
+                regroup_on_vector(1, 0, 0)
+            if k == 3:
+                add_bias(2)
             quantise_s(k)
             if k == 0:
                 quantise_zf(0)
-        transpose_w()
-        quantise_w()
+            if k == 2:
+                shift(0, 0)
+                shift(0, 1)
+            if k == 3:
+                shift(0, 2)
+                shift(0, 3)
 
         for t in range(T_Z3 - 1):
             if t > 0:
                 quantise_z3(t - 1, 4, 8)
                 new_z3(t)
-            for r in range(4):
+            for r in range(4 if t == 0 else 0, 4):
                 shift(t, r)
-            regroup_on_vector(t + 1, 0, 0)
-            regroup_on_vector(t + 1, 1, SCALAR_REGROUP_COLUMNS if t > 0 else 0)
-            new_zf(t + 1)
-            for c in range(4):
-                transpose_z2(t + 1, c)
-            quantise_z3(t, 0, 4)
             if t == 0:
-                add_bias(2)
+                transpose_w()
+            if t > 0:
+                regroup_on_vector(t + 1, 0, 0)
+            regroup_on_vector(t + 1, 1, SCALAR_REGROUP_COLUMNS if t > 0 else 0)
+            for t_next in (4, 5) if t == 3 else (t + 1,):
+                new_zf(t_next)
+                for c in range(4):
+                    transpose_z2(t_next, c)
+            if t == 0:
+                quantise_w()
+            quantise_z3(t, 0, 4)
             quantise_zn(t + 1)
+            early = 2 if t == 0 else 0
+            for r in range(4, 4 + early):
+                shift(t, r)
             taps(t + 2, 0, 4)
             taps(t + 2, 4, 8)
             if t + 2 < T_Z3:
@@ -329,13 +347,10 @@ def tile_stgnnlayer_pb_t_kernel(tc, z2, S, w2, w3, y01, b, out):
                 add_bias(t_out)
                 if t_out < 2:
                     store(t_out, 0, 8)
-            for r in range(4, 8):
+            for r in range(4 + early, 8):
                 shift(t, r)
 
         new_z3(4)
-        new_zf(5)
-        for c in range(4):
-            transpose_z2(5, c)
         quantise_z3(3, 4, 8)
         for r in range(4):
             shift(4, r)

@@ -299,9 +299,8 @@ def tile_stgnnlayer_pb_t_kernel(tc, z2, S, w2, w3, y01, b, out):
             transpose_s(k, 0)
             transpose_s(k, 1)
             if k == 3:
-                regroup_on_vector(1, 0, 0)
-            if k == 3:
                 add_bias(2)
+                regroup_on_vector(1, 0, 0)
             quantise_s(k)
             if k == 0:
                 quantise_zf(0)

from contextlib import ExitStack

import concourse.mybir as mybir
from concourse.masks import make_identity

F32 = mybir.dt.float32
BF16 = mybir.dt.bfloat16
U32 = mybir.dt.uint32
U8 = mybir.dt.uint8
FP8X4 = mybir.dt.float8_e4m3fn_x4
ADD = mybir.AluOpType.add

P = 128
T_OUT = 8
T_Z2 = 6
T_Z3 = 5
NODES = 1024
F_IN = 512
F_OUT = 128
TILES = NODES // P
BANK = 512

FLOPS = 2 * (T_Z3 * NODES * NODES * F_IN + (T_Z2 + T_Z3) * NODES * F_IN * F_OUT)

SCALAR_REGROUP_COLUMNS = 304

BIAS_ADDS_AFTER_ROUND = {0: (3,), 1: (4, 0), 2: (5, 1), 3: (6,)}


def tile_stgnnlayer_pb_t_kernel(tc, z2, S, w2, w3, y01, b, out):
    nc = tc.nc
    with ExitStack() as ctx:
        keep = ctx.enter_context(tc.tile_pool(name="keep", bufs=1))
        two = ctx.enter_context(tc.tile_pool(name="two", bufs=2))
        three = ctx.enter_context(tc.tile_pool(name="three", bufs=3))
        psum = ctx.enter_context(tc.psum_pool(name="psum", bufs=8))
        ctx.enter_context(tc.manual_schedule())

        bias_row = keep.tile([P, F_OUT], BF16, name="bias_row")
        ones = keep.tile([P, P], BF16, name="ones")
        nc.vector.memset(bias_row[:], 0.0)
        nc.vector.memset(ones[:], 1.0)
        ident_f32 = keep.tile([P, P], F32, name="ident_f32")
        make_identity(nc, ident_f32[:])
        sort_f32 = keep.tile([P, P], F32, name="sort_f32")
        nc.vector.tensor_copy(
            out=sort_f32[:].rearrange("p (s a) -> p s a", s=4),
            in_=ident_f32[:].rearrange("p (a s) -> p s a", s=4),
        )
        ident_bf16 = keep.tile([P, P], BF16, name="ident_bf16")
        nc.vector.tensor_copy(out=ident_bf16[:], in_=ident_f32[:])

        z2_rows = [keep.tile([P, 8, F_IN], BF16, name="z2_rows%d" % t) for t in range(T_Z2)]
        s_rows = keep.tile([P, TILES, NODES], BF16, name="s_rows")
        y01_rows = keep.tile([P, T_OUT, TILES * F_OUT], BF16, name="y01_rows")
        y_rows = keep.tile([P, T_OUT, TILES * F_OUT], F32, name="y_rows")
        w2_rows = keep.tile([P, F_IN], BF16, name="w2_rows")
        w3_rows = keep.tile([P, F_IN], BF16, name="w3_rows")
        bias_all = keep.tile([P, F_OUT], F32, name="bias_all")

        def load_z2(t, c_lo, c_hi):
            src = z2[0, t].rearrange("(c p e) f -> p c e f", c=4, p=P, e=2)
            dst = z2_rows[t][:].rearrange("p (c e) f -> p c e f", e=2)
            nc.sync.dma_start(out=dst[:, c_lo:c_hi], in_=src[:, c_lo:c_hi])

        s_view = S.rearrange("(q r) m -> q r m", r=TILES)
        y01_view = y01[0].rearrange("t (q r) o -> q t (r o)", r=TILES)

        for c in range(4):
            load_z2(0, c, c + 1)
        nc.sync.dma_start(out=bias_row[0:1, :], in_=b.unsqueeze(0))
        for k in range(4):
            if k == 3:
                nc.sync.dma_start(out=y01_rows[:, 2:3, :], in_=y01_view[:, 2:3, :])
            nc.sync.dma_start(out=s_rows[:, 2 * k : 2 * k + 2, :], in_=s_view[:, 2 * k : 2 * k + 2, :])
        load_z2(1, 0, 2)
        load_z2(1, 2, 4)
        nc.sync.dma_start(out=w2_rows[:], in_=w2)
        nc.sync.dma_start(out=w3_rows[:], in_=w3)
        nc.sync.dma_start(out=y01_rows[:, 3:4, :], in_=y01_view[:, 3:4, :])
        load_z2(2, 0, 4)
        nc.sync.dma_start(out=y01_rows[:, 4:8, :], in_=y01_view[:, 4:8, :])
        load_z2(3, 0, 4)
        nc.sync.dma_start(out=y01_rows[:, 0:2, :], in_=y01_view[:, 0:2, :])
        load_z2(4, 0, 4)
        load_z2(5, 0, 4)

        s_codes = keep.tile([P, 2048], U32, name="s_codes", align_bytes=64)
        s_scales = keep.tile([P, 2048], U8, name="s_scales", align_bytes=64)
        w2_codes = keep.tile([P, P], U32, name="w2_codes", align_bytes=64)
        w2_scales = keep.tile([P, P], U8, name="w2_scales", align_bytes=64)
        w3_codes = keep.tile([P, P], U32, name="w3_codes", align_bytes=64)
        w3_scales = keep.tile([P, P], U8, name="w3_scales", align_bytes=64)
        s_grouped = {}
        zn_grouped, zn_codes, zn_scales = {}, {}, {}
        zf_grouped, zf_codes, zf_scales = {}, {}, {}
        z3_grouped, z3_codes, z3_scales = {}, {}, {}
        tap_banks = {}

        s_words = s_rows[:].bitcast(F32)

        def transpose_s(k, g):
            if g == 0:
                s_grouped[k] = keep.tile([P, 2048], BF16, name="s_grouped%d" % k, align_bytes=64)
            bank = psum.tile([P, BANK], F32, tag="bank", name="s_bank%d_%d" % (k, g))
            for u in range(2):
                for i in range(2):
                    nc.tensor.transpose(
                        bank[:, u * 256 + i * 128 : u * 256 + i * 128 + 128],
                        s_words[:, 2 * k + i, (2 * g + u) * 128 : (2 * g + u) * 128 + 128],
                        ident_f32[:],
                    )
            nc.scalar.copy(
                out=s_grouped[k][:].bitcast(F32)[:, g * 512 : (g + 1) * 512].rearrange("p (n u) -> p n u", u=2),
                in_=bank[:].rearrange("p (u n) -> p n u", u=2),
            )

        def quantise_s(k):
            nc.vector.quantize_mx(
                out=s_codes[:, k * 512 : (k + 1) * 512].bitcast(FP8X4),
                scales=s_scales[:, k * 512 : (k + 1) * 512],
                in_=s_grouped[k][:],
            )

        w2_grouped = keep.tile([P, F_IN], BF16, name="w2_grouped", align_bytes=64)
        w3_grouped = keep.tile([P, F_IN], BF16, name="w3_grouped", align_bytes=64)

        def transpose_w():
            w2_bank = psum.tile([P, 256], F32, tag="bank", name="w2_bank")
            w2_words = w2_rows[:].bitcast(F32)
            for u in range(2):
                nc.tensor.transpose(
                    w2_bank[:, u * 128 : u * 128 + 128], w2_words[:, u * 128 : u * 128 + 128], ident_f32[:]
                )
            nc.scalar.copy(
                out=w2_grouped[:].bitcast(F32).rearrange("p (o u) -> p o u", u=2),
                in_=w2_bank[:].rearrange("p (u o) -> p o u", u=2),
            )
            w3_bank = psum.tile([P, 512], BF16, tag="bank", name="w3_bank")
            for j in range(4):
                nc.tensor.transpose(
                    w3_bank[:, j * 128 : j * 128 + 128], w3_rows[:, j * 128 : j * 128 + 128], ident_bf16[:]
                )
            nc.scalar.copy(
                out=w3_grouped[:].rearrange("p (o j) -> p o j", j=4),
                in_=w3_bank[:].rearrange("p (j o) -> p o j", j=4),
            )

        def quantise_w():
            nc.vector.quantize_mx(out=w2_codes[:].bitcast(FP8X4), scales=w2_scales[:], in_=w2_grouped[:])
            nc.vector.quantize_mx(out=w3_codes[:].bitcast(FP8X4), scales=w3_scales[:], in_=w3_grouped[:])

        def spread_bias():
            bias_bank = psum.tile([P, F_OUT], F32, tag="bank", name="bias_bank")
            nc.tensor.matmul(out=bias_bank[:], lhsT=ones[:], rhs=bias_row[:], start=True, stop=True)
            nc.scalar.copy(out=bias_all[:], in_=bias_bank[:])

        def new_zf(t):
            zf_grouped[t] = two.tile([P, 4096], BF16, tag="zf_grouped", name="zf_grouped%d" % t, align_bytes=64)
            zf_codes[t] = three.tile([P, 1024], U32, tag="zf_codes", name="zf_codes%d" % t, align_bytes=64)
            zf_scales[t] = three.tile([P, 1024], U8, tag="zf_scales", name="zf_scales%d" % t, align_bytes=64)

        def transpose_z2(t, c):
            z2_words = z2_rows[t][:].bitcast(F32)
            bank = psum.tile([P, BANK], F32, tag="bank", name="zf_bank%d_%d" % (t, c))
            for u in range(2):
                for e in range(2):
                    nc.tensor.transpose(
                        bank[:, u * 256 + e * 128 : u * 256 + e * 128 + 128],
                        z2_words[:, 2 * c + e, u * 128 : u * 128 + 128],
                        sort_f32[:],
                    )
            grouped_words = zf_grouped[t][:].bitcast(F32).rearrange("p (r q u) -> p r q u", r=8, q=128, u=2)
            nc.scalar.copy(
                out=grouped_words[:, :, 32 * c : 32 * c + 32, :],
                in_=bank[:].rearrange("p (u r q) -> p r q u", u=2, r=8, q=32),
            )

        def quantise_zf(t):
            nc.vector.quantize_mx(out=zf_codes[t][:].bitcast(FP8X4), scales=zf_scales[t][:], in_=zf_grouped[t][:])

        def new_zn(t):
            zn_grouped[t] = two.tile([P, 2, 2048], BF16, tag="zn_grouped", name="zn_grouped%d" % t, align_bytes=64)
            zn_codes[t] = two.tile([P, 1024], U32, tag="zn_codes", name="zn_codes%d" % t, align_bytes=64)
            zn_scales[t] = two.tile([P, 1024], U8, tag="zn_scales", name="zn_scales%d" % t, align_bytes=64)

        def regroup_views(t, g):
            dst = zn_grouped[t][:, g, :].rearrange("p (c i j) -> p c j i", i=4, j=4)
            src = z2_rows[t][:, 4 * g : 4 * g + 4, :].rearrange("p j (c i) -> p c j i", i=4)
            return dst, src

        def regroup_on_vector(t, g, scalar_columns):
            dst, src = regroup_views(t, g)
            split = (F_IN - scalar_columns) // 4
            nc.vector.tensor_copy(out=dst[:, 0:split], in_=src[:, 0:split])

        def regroup_on_scalar(t, g, scalar_columns):
            dst, src = regroup_views(t, g)
            split = (F_IN - scalar_columns) // 4
            nc.scalar.copy(out=dst[:, split:128], in_=src[:, split:128])

        def quantise_zn(t):
            nc.vector.quantize_mx(
                out=zn_codes[t][:].bitcast(FP8X4),
                scales=zn_scales[t][:],
                in_=zn_grouped[t][:].rearrange("p g x -> p (g x)"),
            )

        def new_z3(t):
            z3_grouped[t] = two.tile([P, TILES, 512], BF16, tag="z3_grouped", name="z3_grouped%d" % t, align_bytes=64)
            z3_codes[t] = two.tile([P, 1024], U32, tag="z3_codes", name="z3_codes%d" % t, align_bytes=64)
            z3_scales[t] = two.tile([P, 1024], U8, tag="z3_scales", name="z3_scales%d" % t, align_bytes=64)

        def shift(t, r):
            bank = psum.tile([P, BANK], F32, tag="bank", name="z3_bank%d_%d" % (t, r))
            k, i = divmod(r, 2)
            for j in range(4):
                for g in range(2):
                    z_col = g * 512 + j * 128
                    s_col = k * 512 + g * 256 + i * 128
                    nc.tensor.matmul_mx(
                        out=bank[:, j * 128 : j * 128 + 128],
                        lhsT=zn_codes[t][:, z_col : z_col + 128].bitcast(FP8X4),
                        lhsT_scale=zn_scales[t][:, z_col : z_col + 128],
                        rhs=s_codes[:, s_col : s_col + 128].bitcast(FP8X4),
                        rhs_scale=s_scales[:, s_col : s_col + 128],
                        start=(g == 0),
                        stop=(g == 1),
                    )
            nc.scalar.copy(
                out=z3_grouped[t][:, r, :].rearrange("p (q j) -> p q j", j=4),
                in_=bank[:].rearrange("p (j q) -> p q j", j=4),
            )

        def quantise_z3(t, r_lo, r_hi):
            nc.vector.quantize_mx(
                out=z3_codes[t][:, r_lo * 128 : r_hi * 128].bitcast(FP8X4),
                scales=z3_scales[t][:, r_lo * 128 : r_hi * 128],
                in_=z3_grouped[t][:, r_lo:r_hi, :].rearrange("p r x -> p (r x)"),
            )

        def taps(t_out, r_lo, r_hi):
            bank = psum.tile([P, (r_hi - r_lo) * 128], F32, tag="bank", name="tap_bank%d_%d" % (t_out, r_lo))
            tap_banks[(t_out, r_lo)] = bank
            for r in range(r_lo, r_hi):
                col = (r - r_lo) * 128
                zf_col = ((r % 2) * 4 + r // 2) * 128
                nc.tensor.matmul_mx(
                    out=bank[:, col : col + 128],
                    lhsT=zf_codes[t_out - 2][:, zf_col : zf_col + 128].bitcast(FP8X4),
                    lhsT_scale=zf_scales[t_out - 2][:, zf_col : zf_col + 128],
                    rhs=w2_codes[:].bitcast(FP8X4),
                    rhs_scale=w2_scales[:],
                    start=True,
                    stop=(t_out < 3),
                )
                if t_out >= 3:
                    nc.tensor.matmul_mx(
                        out=bank[:, col : col + 128],
                        lhsT=z3_codes[t_out - 3][:, r * 128 : r * 128 + 128].bitcast(FP8X4),
                        lhsT_scale=z3_scales[t_out - 3][:, r * 128 : r * 128 + 128],
                        rhs=w3_codes[:].bitcast(FP8X4),
                        rhs_scale=w3_scales[:],
                        start=False,
                        stop=True,
                    )

        def add_bias(t_out):
            nc.vector.tensor_tensor(
                out=y_rows[:, t_out, :].rearrange("p (r o) -> p r o", o=F_OUT),
                in0=y01_rows[:, t_out, :].rearrange("p (r o) -> p r o", o=F_OUT),
                in1=bias_all[:].unsqueeze(1).to_broadcast([P, TILES, F_OUT]),
                op=ADD,
            )

        def add_taps(t_out, r_lo, r_hi):
            nc.vector.tensor_tensor(
                out=y_rows[:, t_out, r_lo * 128 : r_hi * 128],
                in0=tap_banks[(t_out, r_lo)][:],
                in1=y_rows[:, t_out, r_lo * 128 : r_hi * 128],
                op=ADD,
            )

        def store(t_out, r_lo, r_hi):
            y_view = out[0, t_out].rearrange("(q r) o -> q (r o)", r=TILES)
            nc.sync.dma_start(out=y_view[:, r_lo * 128 : r_hi * 128], in_=y_rows[:, t_out, r_lo * 128 : r_hi * 128])

        new_zf(0)
        new_zn(0)
        for c in range(4):
            transpose_z2(0, c)
        spread_bias()
        regroup_on_vector(0, 0, 0)
        regroup_on_vector(0, 1, 0)
        quantise_zn(0)
        new_zn(1)
        new_z3(0)
        for k in range(4):
            transpose_s(k, 0)
            transpose_s(k, 1)
            if k == 3:
                add_bias(2)
                regroup_on_vector(1, 0, 0)
            quantise_s(k)
            if k == 0:
                quantise_zf(0)
            if k == 2:
                shift(0, 0)
                shift(0, 1)
            if k == 3:
                shift(0, 2)
                shift(0, 3)

        for t in range(T_Z3 - 1):
            if t > 0:
                quantise_z3(t - 1, 4, 8)
                new_z3(t)
            for r in range(4 if t == 0 else 0, 4):
                shift(t, r)
            if t == 0:
                transpose_w()
            if t > 0:
                regroup_on_vector(t + 1, 0, 0)
            regroup_on_vector(t + 1, 1, SCALAR_REGROUP_COLUMNS if t > 0 else 0)
            for t_next in (4, 5) if t == 3 else (t + 1,):
                new_zf(t_next)
                for c in range(4):
                    transpose_z2(t_next, c)
            if t == 0:
                quantise_w()
            quantise_z3(t, 0, 4)
            quantise_zn(t + 1)
            early = 2 if t == 0 else 0
            for r in range(4, 4 + early):
                shift(t, r)
            taps(t + 2, 0, 4)
            taps(t + 2, 4, 8)
            if t + 2 < T_Z3:
                new_zn(t + 2)
                regroup_on_scalar(t + 2, 1, SCALAR_REGROUP_COLUMNS)
            add_taps(t + 2, 0, 4)
            add_taps(t + 2, 4, 8)
            store(t + 2, 0, 8)
            quantise_zf(t + 1)
            for t_out in BIAS_ADDS_AFTER_ROUND[t]:
                add_bias(t_out)
                if t_out < 2:
                    store(t_out, 0, 8)
            for r in range(4 + early, 8):
                shift(t, r)

        new_z3(4)
        quantise_z3(3, 4, 8)
        for r in range(4):
            shift(4, r)
        taps(6, 0, 4)
        for r in range(4, 8):
            shift(4, r)
        add_bias(7)
        quantise_zf(5)
        add_taps(6, 0, 4)
        store(6, 0, 4)
        quantise_z3(4, 0, 4)
        taps(6, 4, 8)
        taps(7, 0, 4)
        quantise_z3(4, 4, 6)
        taps(7, 4, 6)
        quantise_z3(4, 6, 7)
        taps(7, 6, 7)
        add_taps(6, 4, 8)
        store(6, 4, 8)
        quantise_z3(4, 7, 8)
        taps(7, 7, 8)
        add_taps(7, 0, 4)
        store(7, 0, 4)
        add_taps(7, 4, 6)
        store(7, 4, 6)
        add_taps(7, 6, 7)
        add_taps(7, 7, 8)
        store(7, 6, 8)
